import numpy as np
import ml_dtypes


def mxq(x, axis, fmt="e4m3"):
    dtype, down = {"e4m3": (ml_dtypes.float8_e4m3fn, 7), "e5m2": (ml_dtypes.float8_e5m2, 14)}[fmt]
    v = np.moveaxis(np.asarray(x, np.float32).astype(ml_dtypes.bfloat16).astype(np.float64), axis, -1)
    blocks = v.reshape(v.shape[:-1] + (-1, 32))
    amax = np.abs(blocks).max(-1, keepdims=True)
    byte = np.maximum(np.where(amax > 0, np.frexp(amax)[1] - 1 + 127, 0) - down, 1)
    scale = np.exp2(byte - 127.0)
    codes = (blocks / scale).astype(np.float32).astype(dtype).astype(np.float64)
    return np.moveaxis((codes * scale).reshape(v.shape), -1, axis)


BF16 = ml_dtypes.bfloat16


def bf(x):
    return np.asarray(x, np.float32).astype(BF16)


def f64(x):
    return np.asarray(x).astype(np.float64)


M, NI, NO, G, P = 2048, 512, 512, 5, 3
NB = G + P
K = NB * NI


def silu(v):
    return v / (1.0 + np.exp(-v))


def b_spline_basis(x, t):
    xc = np.clip(x, t[P], t[-P - 1])[..., None]
    n_int = t.shape[0] - 1
    b = ((xc >= t[:-1]) & (xc < t[1:])).astype(np.float64)
    for j in range(1, P + 1):
        nv = n_int - j
        ti = t[:nv]
        ti_j = t[j:nv + j]
        ti1 = t[1:nv + 1]
        ti_j1 = t[j + 1:nv + j + 1]
        a1 = (xc - ti) / np.maximum(ti_j - ti, 1e-8)
        a2 = (ti_j1 - xc) / np.maximum(ti_j1 - ti1, 1e-8)
        b = a1 * b[..., :nv] + a2 * b[..., 1:nv + 1]
    return b


def setup_inputs():
    h = 2.0 / G
    grid = np.linspace(-1.0, 1.0, G + 1)
    knots = np.concatenate([grid[0] - h * np.arange(P, 0, -1), grid, grid[-1] + h * np.arange(1, P + 1)])
    x = np.random.standard_normal((M, NI))
    coeff = np.random.standard_normal((NI, NO, NB)) * 2.0 / np.sqrt(NI)
    bw = np.random.uniform(-1.0, 1.0, (NI, NO)) * 1.5 / np.sqrt(NI)
    g = np.random.standard_normal((M, NO)) * np.exp2(np.random.randint(-12, 1, (M, 1)))
    return {"x": bf(x), "coeff": bf(coeff), "base_weight": bf(bw), "knots": bf(knots), "grad_out": bf(g)}


def reference(x, coeff, base_weight, knots, grad_out):
    basis = b_spline_basis(f64(x), f64(knots))
    bq = mxq(basis.transpose(0, 2, 1).reshape(M, K), 0, "e4m3")
    gq = mxq(f64(grad_out), 0, "e5m2")
    d = bq.T @ gq
    return d.reshape(NB, NI, NO).transpose(1, 2, 0)

@@ -1,0 +1,219 @@
+import math
+from contextlib import ExitStack
+
+import concourse.mybir as mybir
+
+F32 = mybir.dt.float32
+BF16 = mybir.dt.bfloat16
+U32 = mybir.dt.uint32
+U8 = mybir.dt.uint8
+E4M3X4 = mybir.dt.float8_e4m3fn_x4
+E5M2X4 = mybir.dt.float8_e5m2_x4
+ALU = mybir.AluOpType
+ACT = mybir.ActivationFunctionType
+
+P = 128
+PACK = 4
+TOKENS = 2048
+NI = 512
+NO = 512
+NB = 8
+PASSES = TOKENS // (P * PACK)
+FLOPS = 2 * TOKENS * NI * NB * NO
+BYTES = 2 * TOKENS * NI + 2 * TOKENS * NO + 4 * NI * NO * NB
+
+KNOTS = (
+    -2.203125,
+    -1.796875,
+    -1.3984375,
+    -1.0,
+    -0.6015625,
+    -0.2001953125,
+    0.2001953125,
+    0.6015625,
+    1.0,
+    1.3984375,
+    1.796875,
+    2.203125,
+)
+
+
+def power_coefficient(r, j):
+    tj = KNOTS[r + j]
+    prod = 1.0
+    for other in range(5):
+        if other != j:
+            prod = prod * (tj - KNOTS[r + other])
+    return (KNOTS[r + 4] - KNOTS[r]) / prod
+
+
+def tile_bsplinekanlayer_kernel(tc, x, coeff, base_weight, knots, grad_out, out):
+    nc = tc.nc
+    t6 = KNOTS[6]
+    t7 = KNOTS[7]
+    HALF = 2
+    W = HALF * P * PACK
+
+    def lead(r, j):
+        return math.sqrt(2.0 * power_coefficient(r, j))
+
+    with ExitStack() as ctx:
+        keep = ctx.enter_context(tc.tile_pool(name="keep", bufs=1))
+        gin = ctx.enter_context(tc.tile_pool(name="gin", bufs=2))
+        small = ctx.enter_context(tc.tile_pool(name="small", bufs=2))
+        upool = ctx.enter_context(tc.tile_pool(name="upool", bufs=4))
+        cpool = ctx.enter_context(tc.tile_pool(name="cpool", bufs=8))
+        tpool = ctx.enter_context(tc.tile_pool(name="tpool", bufs=2))
+        fpool = ctx.enter_context(tc.tile_pool(name="fpool", bufs=8))
+        ppool = ctx.enter_context(tc.tile_pool(name="ppool", bufs=6))
+        opool = ctx.enter_context(tc.tile_pool(name="opool", bufs=4))
+        qpool = ctx.enter_context(tc.tile_pool(name="qpool", bufs=6))
+        rpool = ctx.enter_context(tc.tile_pool(name="rpool", bufs=1))
+        psum = ctx.enter_context(tc.psum_pool(name="psum", bufs=1))
+
+        x_raw = keep.tile([P, PASSES, PACK, NI], BF16)
+        for c in range(PASSES):
+            nc.sync.dma_start(
+                out=x_raw[:, c],
+                in_=x[c * P * PACK : (c + 1) * P * PACK, :].rearrange("(p j) i -> p j i", j=PACK),
+            )
+        g_codes = keep.tile([P, PASSES, NO], U32, align_bytes=64)
+        g_scales = keep.tile([P, PASSES, NO], U8, align_bytes=64)
+
+        def prepare_g():
+            for c in range(PASSES):
+                g_raw = gin.tile([P, PACK, NO], BF16)
+                nc.sync.dma_start(
+                    out=g_raw[:],
+                    in_=grad_out[c * P * PACK : (c + 1) * P * PACK, :].rearrange("(p j) o -> p j o", j=PACK),
+                )
+                g_grp = gin.tile([P, NO, PACK], BF16, align_bytes=64)
+                nc.scalar.copy(out=g_grp[:], in_=g_raw[:].rearrange("p j o -> p o j"))
+                nc.vector.quantize_mx(
+                    out=g_codes[:, c, :].bitcast(E5M2X4),
+                    scales=g_scales[:, c, :],
+                    in_=g_grp[:].rearrange("p o j -> p (o j)"),
+                )
+
+        def relu_cube(z, sign, knot, scale):
+            u = upool.tile([P, W], F32, name="u")
+            nc.scalar.activation(out=u[:], in_=z[:], func=ACT.Relu, bias=-sign * knot, scale=sign)
+            cube = cpool.tile([P, W], F32, name="cube")
+            nc.scalar.activation(out=cube[:], in_=u[:], func=ACT.Square, scale=scale)
+            nc.vector.tensor_tensor(out=cube[:], in0=u[:], in1=cube[:], op=ALU.mult)
+            return cube
+
+        def plain_cube(z, shift, scale):
+            cube = cpool.tile([P, W], F32, name="cube")
+            nc.scalar.activation(out=cube[:], in_=z[:], func=ACT.Square, bias=scale * shift, scale=scale)
+            nc.vector.scalar_tensor_tensor(
+                out=cube[:], in0=z[:], scalar=shift, in1=cube[:], op0=ALU.add, op1=ALU.mult
+            )
+            return cube
+
+        def axpy(dst, a, factor, b, op1):
+            nc.vector.scalar_tensor_tensor(out=dst[:], in0=a[:], scalar=factor, in1=b[:], op0=ALU.mult, op1=op1)
+
+        def basis_unit(b, h):
+            xc = small.tile([P, W], BF16)
+            nc.vector.tensor_scalar(
+                out=xc[:].rearrange("p (c i j) -> p c i j", c=HALF, i=P, j=PACK),
+                in0=x_raw[:, h * HALF : (h + 1) * HALF, :, b * P : (b + 1) * P].rearrange("p c j i -> p c i j"),
+                scalar1=-1.0,
+                scalar2=1.0,
+                op0=ALU.max,
+                op1=ALU.min,
+            )
+            z = small.tile([P, W], BF16)
+            nc.scalar.activation(out=z[:], in_=xc[:], func=ACT.Abs)
+            s_pos = small.tile([P, W], BF16)
+            nc.vector.tensor_scalar(out=s_pos[:], in0=xc[:], scalar1=0.0, scalar2=0.5, op0=ALU.is_ge, op1=ALU.subtract)
+            s_neg = small.tile([P, W], BF16)
+            nc.vector.tensor_scalar(out=s_neg[:], in0=xc[:], scalar1=0.0, scalar2=0.5, op0=ALU.is_lt, op1=ALU.subtract)
+
+            f = {}
+            w6 = relu_cube(z, -1.0, t6, lead(2, 4))
+            w7 = relu_cube(z, -1.0, t7, lead(3, 4))
+            w8n = plain_cube(z, -1.0, lead(4, 4))
+            f[2] = fpool.tile([P, W], BF16, name="f")
+            nc.scalar.copy(out=f[2][:], in_=w6[:])
+            f[3] = fpool.tile([P, W], BF16, name="f")
+            axpy(f[3], w6, power_coefficient(3, 3) / power_coefficient(2, 4), w7, ALU.add)
+            t4 = tpool.tile([P, W], F32, name="t")
+            axpy(t4, w6, power_coefficient(4, 2) / power_coefficient(2, 4), w8n, ALU.subtract)
+            f[4] = fpool.tile([P, W], BF16, name="f")
+            axpy(f[4], w7, power_coefficient(4, 3) / power_coefficient(3, 4), t4, ALU.add)
+            u7 = relu_cube(z, 1.0, t7, lead(7, 0))
+            u6 = relu_cube(z, 1.0, t6, lead(6, 0))
+            u5 = plain_cube(z, t6, lead(5, 0))
+            f[7] = fpool.tile([P, W], BF16, name="f")
+            nc.scalar.copy(out=f[7][:], in_=u7[:])
+            f[6] = fpool.tile([P, W], BF16, name="f")
+            axpy(f[6], u7, power_coefficient(6, 1) / power_coefficient(7, 0), u6, ALU.add)
+            t5 = tpool.tile([P, W], F32, name="t")
+            axpy(t5, u7, power_coefficient(5, 2) / power_coefficient(7, 0), u5, ALU.add)
+            f[5] = fpool.tile([P, W], BF16, name="f")
+            axpy(f[5], u6, power_coefficient(5, 1) / power_coefficient(6, 0), t5, ALU.add)
+
+            done = []
+            for hi, lo in ((7, 0), (6, 1), (5, 2), (4, 3)):
+                pair = opool.tile([P, 2, W], BF16, name="pair", align_bytes=64)
+                p_hi = ppool.tile([P, W], BF16, name="p")
+                nc.vector.tensor_tensor(out=p_hi[:], in0=f[hi][:], in1=s_pos[:], op=ALU.mult)
+                if lo < 2:
+                    nc.vector.tensor_scalar(
+                        out=pair[:, 0, :], in0=p_hi[:], scalar1=0.0, scalar2=None, op0=ALU.max
+                    )
+                    nc.vector.tensor_scalar(
+                        out=pair[:, 1, :], in0=p_hi[:], scalar1=-1.0, scalar2=0.0, op0=ALU.mult, op1=ALU.max
+                    )
+                else:
+                    n_lo = ppool.tile([P, W], BF16, name="p")
+                    nc.vector.tensor_tensor(out=n_lo[:], in0=f[lo][:], in1=s_neg[:], op=ALU.mult)
+                    nc.vector.tensor_tensor(out=pair[:, 0, :], in0=p_hi[:], in1=n_lo[:], op=ALU.max)
+                    nc.vector.tensor_tensor(out=n_lo[:], in0=p_hi[:], in1=n_lo[:], op=ALU.min)
+                    nc.vector.tensor_scalar(
+                        out=pair[:, 1, :], in0=n_lo[:], scalar1=-1.0, scalar2=None, op0=ALU.mult
+                    )
+                codes = qpool.tile([P, 2 * W // PACK], U32, name="codes", align_bytes=64)
+                scales = qpool.tile([P, 2 * W // PACK], U8, name="scales", align_bytes=64)
+                nc.vector.quantize_mx(
+                    out=codes[:].bitcast(E4M3X4), scales=scales[:], in_=pair[:].rearrange("p r n -> p (r n)")
+                )
+                done.append((codes, scales, (hi, lo)))
+            return done
+
+        first = True
+        for b in range(NI // P):
+            acc = [psum.tile([P, NO], F32, name="acc%d" % r) for r in range(NB)]
+            for h in range(PASSES // HALF):
+                done = basis_unit(b, h)
+                if first:
+                    prepare_g()
+                    first = False
+                for codes, scales, pair_r in done:
+                    for k in range(2):
+                        for ci in range(HALF):
+                            c = h * HALF + ci
+                            cols = slice((k * HALF + ci) * P, (k * HALF + ci + 1) * P)
+                            nc.tensor.matmul_mx(
+                                out=acc[pair_r[k]][:],
+                                lhsT=codes[:, cols].bitcast(E4M3X4),
+                                lhsT_scale=scales[:, cols],
+                                rhs=g_codes[:, c, :].bitcast(E5M2X4),
+                                rhs_scale=g_scales[:, c, :],
+                                start=(c == 0),
+                                stop=(c == PASSES - 1),
+                            )
+            planes = rpool.tile([P, NB, NO], F32)
+            for r in range(NB):
+                nc.scalar.copy(out=planes[:, r, :], in_=acc[r][:])
+            woven = rpool.tile([P, NO, NB], F32)
+            for oh in range(2):
+                o_cols = slice(oh * NO // 2, (oh + 1) * NO // 2)
+                for rq in range(2):
+                    r_rows = slice(rq * 4, (rq + 1) * 4)
+                    nc.scalar.copy(
+                        out=woven[:, o_cols, r_rows], in_=planes[:, r_rows, o_cols].rearrange("p r o -> p o r")
+                    )
+                nc.sync.dma_start(out=out[b * P : (b + 1) * P, o_cols, :], in_=woven[:, o_cols, :])

@@ -53,167 +53,243 @@ def tile_bsplinekanlayer_kernel(tc, x, coeff, base_weight, knots, grad_out, out)
     t7 = KNOTS[7]
     HALF = 2
     W = HALF * P * PACK
+    BLOCKS = NI // P
+    UNITS = BLOCKS * PASSES // HALF
+    PER_BLOCK = PASSES // HALF
 
-    def lead(r, j):
-        return math.sqrt(2.0 * power_coefficient(r, j))
+    def c2(r, j):
+        return 2.0 * power_coefficient(r, j)
 
     with ExitStack() as ctx:
+        ctx.enter_context(tc.manual_schedule())
         keep = ctx.enter_context(tc.tile_pool(name="keep", bufs=1))
-        gin = ctx.enter_context(tc.tile_pool(name="gin", bufs=2))
-        small = ctx.enter_context(tc.tile_pool(name="small", bufs=2))
-        upool = ctx.enter_context(tc.tile_pool(name="upool", bufs=4))
-        cpool = ctx.enter_context(tc.tile_pool(name="cpool", bufs=8))
-        tpool = ctx.enter_context(tc.tile_pool(name="tpool", bufs=2))
-        fpool = ctx.enter_context(tc.tile_pool(name="fpool", bufs=8))
-        ppool = ctx.enter_context(tc.tile_pool(name="ppool", bufs=6))
-        opool = ctx.enter_context(tc.tile_pool(name="opool", bufs=4))
-        qpool = ctx.enter_context(tc.tile_pool(name="qpool", bufs=6))
-        rpool = ctx.enter_context(tc.tile_pool(name="rpool", bufs=1))
+        two = ctx.enter_context(tc.tile_pool(name="two", bufs=2))
+        three = ctx.enter_context(tc.tile_pool(name="three", bufs=3))
+        upool = ctx.enter_context(tc.tile_pool(name="upool", bufs=6))
         psum = ctx.enter_context(tc.psum_pool(name="psum", bufs=1))
 
         x_raw = keep.tile([P, PASSES, PACK, NI], BF16)
+        g_codes = keep.tile([P, PASSES, NO], U32, align_bytes=64)
+        g_scales = keep.tile([P, PASSES, NO], U8, align_bytes=64)
+        g_raw = keep.tile([P, PASSES, PACK, NO], BF16, tag="planes", align_bytes=64)
+        g_grp = keep.tile([P, PASSES, NO, PACK], BF16, tag="woven", align_bytes=64)
         for c in range(PASSES):
             nc.sync.dma_start(
                 out=x_raw[:, c],
                 in_=x[c * P * PACK : (c + 1) * P * PACK, :].rearrange("(p j) i -> p j i", j=PACK),
             )
-        g_codes = keep.tile([P, PASSES, NO], U32, align_bytes=64)
-        g_scales = keep.tile([P, PASSES, NO], U8, align_bytes=64)
-
-        def prepare_g():
-            for c in range(PASSES):
-                g_raw = gin.tile([P, PACK, NO], BF16)
-                nc.sync.dma_start(
-                    out=g_raw[:],
-                    in_=grad_out[c * P * PACK : (c + 1) * P * PACK, :].rearrange("(p j) o -> p j o", j=PACK),
-                )
-                g_grp = gin.tile([P, NO, PACK], BF16, align_bytes=64)
-                nc.scalar.copy(out=g_grp[:], in_=g_raw[:].rearrange("p j o -> p o j"))
-                nc.vector.quantize_mx(
-                    out=g_codes[:, c, :].bitcast(E5M2X4),
-                    scales=g_scales[:, c, :],
-                    in_=g_grp[:].rearrange("p o j -> p (o j)"),
-                )
-
-        def relu_cube(z, sign, knot, scale):
-            u = upool.tile([P, W], F32, name="u")
-            nc.scalar.activation(out=u[:], in_=z[:], func=ACT.Relu, bias=-sign * knot, scale=sign)
-            cube = cpool.tile([P, W], F32, name="cube")
-            nc.scalar.activation(out=cube[:], in_=u[:], func=ACT.Square, scale=scale)
-            nc.vector.tensor_tensor(out=cube[:], in0=u[:], in1=cube[:], op=ALU.mult)
-            return cube
-
-        def plain_cube(z, shift, scale):
-            cube = cpool.tile([P, W], F32, name="cube")
-            nc.scalar.activation(out=cube[:], in_=z[:], func=ACT.Square, bias=scale * shift, scale=scale)
-            nc.vector.scalar_tensor_tensor(
-                out=cube[:], in0=z[:], scalar=shift, in1=cube[:], op0=ALU.add, op1=ALU.mult
+        for c in range(PASSES):
+            nc.sync.dma_start(
+                out=g_raw[:, c],
+                in_=grad_out[c * P * PACK : (c + 1) * P * PACK, :].rearrange("(p j) o -> p j o", j=PACK),
             )
-            return cube
+
+        def prepare_g(c):
+            nc.vector.tensor_copy(out=g_grp[:, c], in_=g_raw[:, c].rearrange("p j o -> p o j"))
+            nc.vector.quantize_mx(
+                out=g_codes[:, c, :].bitcast(E5M2X4),
+                scales=g_scales[:, c, :],
+                in_=g_grp[:, c].rearrange("p o j -> p (o j)"),
+            )
+
+        tiles = [dict() for u in range(UNITS)]
+        acc = {}
+        CUBES = (("y7", -t7, 1.0), ("y6", -t6, 1.0), ("y5", t6, math.sqrt(c2(5, 0))), ("y8", -1.0, math.sqrt(c2(4, 4))))
 
         def axpy(dst, a, factor, b, op1):
-            nc.vector.scalar_tensor_tensor(out=dst[:], in0=a[:], scalar=factor, in1=b[:], op0=ALU.mult, op1=op1)
+            nc.vector.scalar_tensor_tensor(out=dst, in0=a[:], scalar=factor, in1=b[:], op0=ALU.mult, op1=op1)
 
-        def basis_unit(b, h):
-            xc = small.tile([P, W], BF16)
+        def clip_and_sign(u):
+            t = tiles[u]
+            b = u // PER_BLOCK
+            h = u % PER_BLOCK
+            t["xc"] = two.tile([P, W], BF16, name="xc")
             nc.vector.tensor_scalar(
-                out=xc[:].rearrange("p (c i j) -> p c i j", c=HALF, i=P, j=PACK),
+                out=t["xc"][:].rearrange("p (c i j) -> p c i j", c=HALF, i=P, j=PACK),
                 in0=x_raw[:, h * HALF : (h + 1) * HALF, :, b * P : (b + 1) * P].rearrange("p c j i -> p c i j"),
                 scalar1=-1.0,
                 scalar2=1.0,
                 op0=ALU.max,
                 op1=ALU.min,
             )
-            z = small.tile([P, W], BF16)
-            nc.scalar.activation(out=z[:], in_=xc[:], func=ACT.Abs)
-            s_pos = small.tile([P, W], BF16)
-            nc.vector.tensor_scalar(out=s_pos[:], in0=xc[:], scalar1=0.0, scalar2=0.5, op0=ALU.is_ge, op1=ALU.subtract)
-            s_neg = small.tile([P, W], BF16)
-            nc.vector.tensor_scalar(out=s_neg[:], in0=xc[:], scalar1=0.0, scalar2=0.5, op0=ALU.is_lt, op1=ALU.subtract)
+            t["s"] = three.tile([P, W], BF16, name="s")
+            nc.vector.tensor_scalar(
+                out=t["s"][:], in0=t["xc"][:], scalar1=0.0, scalar2=0.5, op0=ALU.is_ge, op1=ALU.subtract
+            )
 
-            f = {}
-            w6 = relu_cube(z, -1.0, t6, lead(2, 4))
-            w7 = relu_cube(z, -1.0, t7, lead(3, 4))
-            w8n = plain_cube(z, -1.0, lead(4, 4))
-            f[2] = fpool.tile([P, W], BF16, name="f")
-            nc.scalar.copy(out=f[2][:], in_=w6[:])
-            f[3] = fpool.tile([P, W], BF16, name="f")
-            axpy(f[3], w6, power_coefficient(3, 3) / power_coefficient(2, 4), w7, ALU.add)
-            t4 = tpool.tile([P, W], F32, name="t")
-            axpy(t4, w6, power_coefficient(4, 2) / power_coefficient(2, 4), w8n, ALU.subtract)
-            f[4] = fpool.tile([P, W], BF16, name="f")
-            axpy(f[4], w7, power_coefficient(4, 3) / power_coefficient(3, 4), t4, ALU.add)
-            u7 = relu_cube(z, 1.0, t7, lead(7, 0))
-            u6 = relu_cube(z, 1.0, t6, lead(6, 0))
-            u5 = plain_cube(z, t6, lead(5, 0))
-            f[7] = fpool.tile([P, W], BF16, name="f")
-            nc.scalar.copy(out=f[7][:], in_=u7[:])
-            f[6] = fpool.tile([P, W], BF16, name="f")
-            axpy(f[6], u7, power_coefficient(6, 1) / power_coefficient(7, 0), u6, ALU.add)
-            t5 = tpool.tile([P, W], F32, name="t")
-            axpy(t5, u7, power_coefficient(5, 2) / power_coefficient(7, 0), u5, ALU.add)
-            f[5] = fpool.tile([P, W], BF16, name="f")
-            axpy(f[5], u6, power_coefficient(5, 1) / power_coefficient(6, 0), t5, ALU.add)
+        def squares(u):
+            t = tiles[u]
+            t["z"] = two.tile([P, W], BF16, name="z")
+            nc.scalar.activation(out=t["z"][:], in_=t["xc"][:], func=ACT.Abs)
+            for name, shift, scale in CUBES:
+                t[name] = two.tile([P, W], F32, name=name)
+                nc.scalar.activation(out=t[name][:], in_=t["z"][:], func=ACT.Square, bias=scale * shift, scale=scale)
 
-            done = []
-            for hi, lo in ((7, 0), (6, 1), (5, 2), (4, 3)):
-                pair = opool.tile([P, 2, W], BF16, name="pair", align_bytes=64)
-                p_hi = ppool.tile([P, W], BF16, name="p")
-                nc.vector.tensor_tensor(out=p_hi[:], in0=f[hi][:], in1=s_pos[:], op=ALU.mult)
-                if lo < 2:
-                    nc.vector.tensor_scalar(
-                        out=pair[:, 0, :], in0=p_hi[:], scalar1=0.0, scalar2=None, op0=ALU.max
-                    )
-                    nc.vector.tensor_scalar(
-                        out=pair[:, 1, :], in0=p_hi[:], scalar1=-1.0, scalar2=0.0, op0=ALU.mult, op1=ALU.max
-                    )
-                else:
-                    n_lo = ppool.tile([P, W], BF16, name="p")
-                    nc.vector.tensor_tensor(out=n_lo[:], in0=f[lo][:], in1=s_neg[:], op=ALU.mult)
-                    nc.vector.tensor_tensor(out=pair[:, 0, :], in0=p_hi[:], in1=n_lo[:], op=ALU.max)
-                    nc.vector.tensor_tensor(out=n_lo[:], in0=p_hi[:], in1=n_lo[:], op=ALU.min)
-                    nc.vector.tensor_scalar(
-                        out=pair[:, 1, :], in0=n_lo[:], scalar1=-1.0, scalar2=None, op0=ALU.mult
-                    )
-                codes = qpool.tile([P, 2 * W // PACK], U32, name="codes", align_bytes=64)
-                scales = qpool.tile([P, 2 * W // PACK], U8, name="scales", align_bytes=64)
-                nc.vector.quantize_mx(
-                    out=codes[:].bitcast(E4M3X4), scales=scales[:], in_=pair[:].rearrange("p r n -> p (r n)")
+        def cubes(u):
+            t = tiles[u]
+            for name, shift, scale in CUBES:
+                nc.vector.scalar_tensor_tensor(
+                    out=t[name][:], in0=t["z"][:], scalar=shift, in1=t[name][:], op0=ALU.add, op1=ALU.mult
                 )
-                done.append((codes, scales, (hi, lo)))
-            return done
 
-        first = True
-        for b in range(NI // P):
-            acc = [psum.tile([P, NO], F32, name="acc%d" % r) for r in range(NB)]
-            for h in range(PASSES // HALF):
-                done = basis_unit(b, h)
-                if first:
-                    prepare_g()
-                    first = False
-                for codes, scales, pair_r in done:
-                    for k in range(2):
-                        for ci in range(HALF):
-                            c = h * HALF + ci
-                            cols = slice((k * HALF + ci) * P, (k * HALF + ci + 1) * P)
-                            nc.tensor.matmul_mx(
-                                out=acc[pair_r[k]][:],
-                                lhsT=codes[:, cols].bitcast(E4M3X4),
-                                lhsT_scale=scales[:, cols],
-                                rhs=g_codes[:, c, :].bitcast(E5M2X4),
-                                rhs_scale=g_scales[:, c, :],
-                                start=(c == 0),
-                                stop=(c == PASSES - 1),
-                            )
-            planes = rpool.tile([P, NB, NO], F32)
-            for r in range(NB):
-                nc.scalar.copy(out=planes[:, r, :], in_=acc[r][:])
-            woven = rpool.tile([P, NO, NB], F32)
-            for oh in range(2):
-                o_cols = slice(oh * NO // 2, (oh + 1) * NO // 2)
+        def relus(u):
+            t = tiles[u]
+            t["f_out"] = two.tile([P, 2, W], BF16, name="f_out")
+            t["f_lo"] = two.tile([P, 2, W], BF16, name="f_lo")
+            for name in ("u7", "u6", "w6", "w7"):
+                t[name] = upool.tile([P, W], F32, name="u")
+            nc.scalar.activation(out=t["u7"][:], in_=t["y7"][:], func=ACT.Relu, scale=c2(7, 0))
+            nc.scalar.activation(out=t["f_out"][:, 0, :], in_=t["y7"][:], func=ACT.Relu, scale=c2(7, 0))
+            nc.scalar.activation(out=t["u6"][:], in_=t["y6"][:], func=ACT.Relu, scale=c2(6, 0))
+            nc.scalar.activation(out=t["w6"][:], in_=t["y6"][:], func=ACT.Relu, scale=-c2(2, 4))
+            nc.scalar.mul(out=t["f_lo"][:, 0, :], in_=t["w6"][:], mul=-1.0)
+            nc.scalar.activation(out=t["w7"][:], in_=t["y7"][:], func=ACT.Relu, scale=-c2(3, 4))
+
+        def combine_a(u, all_on_vector):
+            t = tiles[u]
+            t["t5"] = two.tile([P, W], F32, name="t5")
+            axpy(t["t5"][:], t["u7"], c2(5, 2) / c2(7, 0), t["y5"], ALU.add)
+            t["t4"] = two.tile([P, W], F32, name="t4")
+            axpy(t["t4"][:], t["w6"], c2(4, 2) / c2(2, 4), t["y8"], ALU.subtract)
+            axpy(t["f_out"][:, 1, :], t["u7"], c2(6, 1) / c2(7, 0), t["u6"], ALU.add)
+            s2 = t["s"][:].unsqueeze(1).to_broadcast([P, 2, W])
+            t["p_out"] = two.tile([P, 2, W], BF16, name="p_out")
+            nc.vector.tensor_tensor(out=t["p_out"][:], in0=t["f_out"][:], in1=s2, op=ALU.mult)
+            t["four_a"] = three.tile([P, 4, W], BF16, name="four", align_bytes=64)
+            nc.vector.tensor_scalar(
+                out=t["four_a"][:, 0:2, :], in0=t["p_out"][:], scalar1=0.0, scalar2=None, op0=ALU.max
+            )
+            if all_on_vector:
+                nc.vector.tensor_scalar(
+                    out=t["four_a"][:, 2:4, :], in0=t["p_out"][:], scalar1=-1.0, scalar2=0.0, op0=ALU.mult, op1=ALU.max
+                )
+
+        def combine_b(u):
+            t = tiles[u]
+            t["f_hi"] = keep.tile([P, 2, W], BF16, name="f_hi")
+            axpy(t["f_hi"][:, 0, :], t["u6"], c2(5, 1) / c2(6, 0), t["t5"], ALU.add)
+            axpy(t["f_hi"][:, 1, :], t["w7"], c2(4, 3) / c2(3, 4), t["t4"], ALU.add)
+            axpy(t["f_lo"][:, 1, :], t["w6"], -c2(3, 3) / c2(2, 4), t["w7"], ALU.subtract)
+            s2 = t["s"][:].unsqueeze(1).to_broadcast([P, 2, W])
+            t["p_hi"] = keep.tile([P, 2, W], BF16, name="p_hi")
+            nc.vector.tensor_tensor(out=t["p_hi"][:], in0=t["f_hi"][:], in1=s2, op=ALU.mult)
+            t["n_lo"] = two.tile([P, 2, W], BF16, name="n_lo")
+            nc.vector.tensor_tensor(out=t["n_lo"][:], in0=t["f_lo"][:], in1=s2, op=ALU.mult)
+            t["four_b"] = three.tile([P, 4, W], BF16, name="four", align_bytes=64)
+            nc.vector.tensor_tensor(out=t["four_b"][:, 0:2, :], in0=t["p_hi"][:], in1=t["n_lo"][:], op=ALU.max)
+
+        def combine_c(u, all_on_vector):
+            t = tiles[u]
+            nc.vector.tensor_tensor(out=t["n_lo"][:], in0=t["p_hi"][:], in1=t["n_lo"][:], op=ALU.min)
+            if all_on_vector:
+                nc.vector.tensor_scalar(
+                    out=t["four_b"][:, 2:4, :], in0=t["n_lo"][:], scalar1=-1.0, scalar2=None, op0=ALU.mult
+                )
+
+        def mirror_on_scalar(u):
+            t = tiles[u]
+            nc.scalar.activation(out=t["four_a"][:, 2:4, :], in_=t["p_out"][:], func=ACT.Relu, scale=-1.0)
+            nc.scalar.mul(out=t["four_b"][:, 2:4, :], in_=t["n_lo"][:], mul=-1.0)
+
+        def quantise_and_multiply(u, which, rs, pieces):
+            t = tiles[u]
+            b = u // PER_BLOCK
+            h = u % PER_BLOCK
+            if h == 0 and which == "four_a":
+                for r in range(NB):
+                    acc[r] = psum.tile([P, NO], F32, name="acc%d" % r)
+            key = "codes_" + which
+            if key not in t:
+                t[key] = three.tile([P, W], U32, name="codes", align_bytes=64)
+                t["scales_" + which] = three.tile([P, W], U8, name="scales", align_bytes=64)
+            codes = t[key]
+            scales = t["scales_" + which]
+            for first, count in pieces:
+                words = slice(first * W // 4, (first + count) * W // 4)
+                nc.vector.quantize_mx(
+                    out=codes[:, words].bitcast(E4M3X4),
+                    scales=scales[:, words],
+                    in_=t[which][:, first : first + count, :].rearrange("p r n -> p (r n)"),
+                )
+                for k in range(first, first + count):
+                    for ci in range(HALF):
+                        c = h * HALF + ci
+                        cols = slice((k * HALF + ci) * P, (k * HALF + ci + 1) * P)
+                        nc.tensor.matmul_mx(
+                            out=acc[rs[k]][:],
+                            lhsT=codes[:, cols].bitcast(E4M3X4),
+                            lhsT_scale=scales[:, cols],
+                            rhs=g_codes[:, c, :].bitcast(E5M2X4),
+                            rhs_scale=g_scales[:, c, :],
+                            start=(c == 0),
+                            stop=(c == PASSES - 1),
+                        )
+
+        RS_A = (7, 6, 0, 1)
+        RS_B = (5, 4, 2, 3)
+        planes = {}
+
+        def empty_banks(b, rs, engines):
+            if b not in planes:
+                planes[b] = keep.tile([P, NB, NO], F32, tag="planes", name="planes", align_bytes=64)
+            for n, r in enumerate(rs):
+                if engines[n % len(engines)] == "v":
+                    nc.vector.tensor_copy(out=planes[b][:, r, :], in_=acc[r][:])
+                else:
+                    nc.scalar.copy(out=planes[b][:, r, :], in_=acc[r][:])
+
+        def weave_and_store(b, engines, stores):
+            woven = keep.tile([P, NO, NB], F32, tag="woven", name="woven", align_bytes=64)
+            quarter = NO // 4
+            for oq in range(4):
+                o_cols = slice(oq * quarter, (oq + 1) * quarter)
                 for rq in range(2):
                     r_rows = slice(rq * 4, (rq + 1) * 4)
-                    nc.scalar.copy(
-                        out=woven[:, o_cols, r_rows], in_=planes[:, r_rows, o_cols].rearrange("p r o -> p o r")
-                    )
-                nc.sync.dma_start(out=out[b * P : (b + 1) * P, o_cols, :], in_=woven[:, o_cols, :])
+                    src = planes[b][:, r_rows, o_cols].rearrange("p r o -> p o r")
+                    if engines[oq % len(engines)] == "v":
+                        nc.vector.tensor_copy(out=woven[:, o_cols, r_rows], in_=src)
+                    else:
+                        nc.scalar.copy(out=woven[:, o_cols, r_rows], in_=src)
+                step = 4 // stores
+                if (oq + 1) % step == 0:
+                    o_st = slice((oq + 1 - step) * quarter, (oq + 1) * quarter)
+                    nc.sync.dma_start(out=out[b * P : (b + 1) * P, o_st, :], in_=woven[:, o_st, :])
+
+        clip_and_sign(0)
+        clip_and_sign(1)
+        squares(0)
+        squares(1)
+        cubes(0)
+        for c in range(PASSES):
+            prepare_g(c)
+        for t in range(UNITS):
+            final = t == UNITS - 1
+            if t + 2 < UNITS:
+                clip_and_sign(t + 2)
+            relus(t)
+            if t >= 1:
+                mirror_on_scalar(t - 1)
+            if t + 2 < UNITS:
+                squares(t + 2)
+            if t >= 3 and t % PER_BLOCK == 1:
+                empty_banks((t - 3) // PER_BLOCK, RS_A + RS_B, "s")
+            if t >= 4 and t % PER_BLOCK == 0:
+                weave_and_store((t - 4) // PER_BLOCK, "s", 2)
+            if t + 1 < UNITS:
+                cubes(t + 1)
+            combine_a(t, final)
+            if t >= 1:
+                quantise_and_multiply(t - 1, "four_a", RS_A, ((0, 4),))
+                quantise_and_multiply(t - 1, "four_b", RS_B, ((0, 4),))
+            if final:
+                quantise_and_multiply(t, "four_a", RS_A, ((0, 4),))
+                weave_and_store(BLOCKS - 2, "s", 2)
+                empty_banks(BLOCKS - 1, RS_A, "s")
+            combine_b(t)
+            if final:
+                quantise_and_multiply(t, "four_b", RS_B, ((0, 2),))
+            combine_c(t, final)
+            if final:
+                quantise_and_multiply(t, "four_b", RS_B, ((2, 2),))
+                empty_banks(BLOCKS - 1, RS_B, "sv")
+                weave_and_store(BLOCKS - 1, "vs", 4)

@@ -2,6 +2,7 @@ import math
 from contextlib import ExitStack
 
 import concourse.mybir as mybir
+from concourse.masks import make_identity
 
 F32 = mybir.dt.float32
 BF16 = mybir.dt.bfloat16
@@ -66,7 +67,9 @@ def tile_bsplinekanlayer_kernel(tc, x, coeff, base_weight, knots, grad_out, out)
         two = ctx.enter_context(tc.tile_pool(name="two", bufs=2))
         three = ctx.enter_context(tc.tile_pool(name="three", bufs=3))
         upool = ctx.enter_context(tc.tile_pool(name="upool", bufs=6))
-        psum = ctx.enter_context(tc.psum_pool(name="psum", bufs=1))
+        four_bufs = ctx.enter_context(tc.tile_pool(name="four_bufs", bufs=4))
+        psum = ctx.enter_context(tc.psum_pool(name="psum", bufs=6))
+        psum_sum = ctx.enter_context(tc.psum_pool(name="psum_sum", bufs=2))
 
         x_raw = keep.tile([P, PASSES, PACK, NI], BF16)
         g_codes = keep.tile([P, PASSES, NO], U32, align_bytes=64)
@@ -83,6 +86,11 @@ def tile_bsplinekanlayer_kernel(tc, x, coeff, base_weight, knots, grad_out, out)
                 out=g_raw[:, c],
                 in_=grad_out[c * P * PACK : (c + 1) * P * PACK, :].rearrange("(p j) o -> p j o", j=PACK),
             )
+
+        diag = [keep.tile([P, P], F32, name="diag%d" % n) for n in range(3)]
+        make_identity(nc, diag[0][:])
+        nc.scalar.mul(out=diag[1][:], in_=diag[0][:], mul=c2(5, 1) / c2(6, 0))
+        nc.scalar.mul(out=diag[2][:], in_=diag[0][:], mul=c2(5, 2) / c2(7, 0))
 
         def prepare_g(c):
             nc.vector.tensor_copy(out=g_grp[:, c], in_=g_raw[:, c].rearrange("p j o -> p o j"))
@@ -145,10 +153,18 @@ def tile_bsplinekanlayer_kernel(tc, x, coeff, base_weight, knots, grad_out, out)
             nc.scalar.mul(out=t["f_lo"][:, 0, :], in_=t["w6"][:], mul=-1.0)
             nc.scalar.activation(out=t["w7"][:], in_=t["y7"][:], func=ACT.Relu, scale=-c2(3, 4))
 
+        def add_function_5(u):
+            t = tiles[u]
+            t["sum5"] = []
+            for n in range(W // NO):
+                cols = slice(n * NO, (n + 1) * NO)
+                bank = psum_sum.tile([P, NO], F32, name="sum5")
+                for k, name in enumerate(("y5", "u6", "u7")):
+                    nc.tensor.matmul(out=bank[:], lhsT=diag[k][:], rhs=t[name][:, cols], start=(k == 0), stop=(k == 2))
+                t["sum5"].append(bank)
+
         def combine_a(u, all_on_vector):
             t = tiles[u]
-            t["t5"] = two.tile([P, W], F32, name="t5")
-            axpy(t["t5"][:], t["u7"], c2(5, 2) / c2(7, 0), t["y5"], ALU.add)
             t["t4"] = two.tile([P, W], F32, name="t4")
             axpy(t["t4"][:], t["w6"], c2(4, 2) / c2(2, 4), t["y8"], ALU.subtract)
             axpy(t["f_out"][:, 1, :], t["u7"], c2(6, 1) / c2(7, 0), t["u6"], ALU.add)
@@ -166,13 +182,15 @@ def tile_bsplinekanlayer_kernel(tc, x, coeff, base_weight, knots, grad_out, out)
 
         def combine_b(u):
             t = tiles[u]
-            t["f_hi"] = keep.tile([P, 2, W], BF16, name="f_hi")
-            axpy(t["f_hi"][:, 0, :], t["u6"], c2(5, 1) / c2(6, 0), t["t5"], ALU.add)
-            axpy(t["f_hi"][:, 1, :], t["w7"], c2(4, 3) / c2(3, 4), t["t4"], ALU.add)
+            t["f4"] = keep.tile([P, W], BF16, name="f4")
+            axpy(t["f4"][:], t["w7"], c2(4, 3) / c2(3, 4), t["t4"], ALU.add)
             axpy(t["f_lo"][:, 1, :], t["w6"], -c2(3, 3) / c2(2, 4), t["w7"], ALU.subtract)
             s2 = t["s"][:].unsqueeze(1).to_broadcast([P, 2, W])
             t["p_hi"] = keep.tile([P, 2, W], BF16, name="p_hi")
-            nc.vector.tensor_tensor(out=t["p_hi"][:], in0=t["f_hi"][:], in1=s2, op=ALU.mult)
+            for n in range(W // NO):
+                cols = slice(n * NO, (n + 1) * NO)
+                nc.vector.tensor_tensor(out=t["p_hi"][:, 0, cols], in0=t["sum5"][n][:], in1=t["s"][:, cols], op=ALU.mult)
+            nc.vector.tensor_tensor(out=t["p_hi"][:, 1, :], in0=t["f4"][:], in1=t["s"][:], op=ALU.mult)
             t["n_lo"] = two.tile([P, 2, W], BF16, name="n_lo")
             nc.vector.tensor_tensor(out=t["n_lo"][:], in0=t["f_lo"][:], in1=s2, op=ALU.mult)
             t["four_b"] = three.tile([P, 4, W], BF16, name="four", align_bytes=64)
@@ -191,39 +209,37 @@ def tile_bsplinekanlayer_kernel(tc, x, coeff, base_weight, knots, grad_out, out)
             nc.scalar.activation(out=t["four_a"][:, 2:4, :], in_=t["p_out"][:], func=ACT.Relu, scale=-1.0)
             nc.scalar.mul(out=t["four_b"][:, 2:4, :], in_=t["n_lo"][:], mul=-1.0)
 
-        def quantise_and_multiply(u, which, rs, pieces):
+        def multiply(u, which, rs, ks):
             t = tiles[u]
-            b = u // PER_BLOCK
             h = u % PER_BLOCK
-            if h == 0 and which == "four_a":
-                for r in range(NB):
-                    acc[r] = psum.tile([P, NO], F32, name="acc%d" % r)
+            for k in ks:
+                if h == 0:
+                    acc[rs[k]] = psum.tile([P, NO], F32, name="acc")
+                for ci in range(HALF):
+                    c = h * HALF + ci
+                    cols = slice((k * HALF + ci) * P, (k * HALF + ci + 1) * P)
+                    nc.tensor.matmul_mx(
+                        out=acc[rs[k]][:],
+                        lhsT=t["codes_" + which][:, cols].bitcast(E4M3X4),
+                        lhsT_scale=t["scales_" + which][:, cols],
+                        rhs=g_codes[:, c, :].bitcast(E5M2X4),
+                        rhs_scale=g_scales[:, c, :],
+                        start=(c == 0),
+                        stop=(c == PASSES - 1),
+                    )
+
+        def quantise(u, which, first, count):
+            t = tiles[u]
             key = "codes_" + which
             if key not in t:
-                t[key] = three.tile([P, W], U32, name="codes", align_bytes=64)
-                t["scales_" + which] = three.tile([P, W], U8, name="scales", align_bytes=64)
-            codes = t[key]
-            scales = t["scales_" + which]
-            for first, count in pieces:
-                words = slice(first * W // 4, (first + count) * W // 4)
-                nc.vector.quantize_mx(
-                    out=codes[:, words].bitcast(E4M3X4),
-                    scales=scales[:, words],
-                    in_=t[which][:, first : first + count, :].rearrange("p r n -> p (r n)"),
-                )
-                for k in range(first, first + count):
-                    for ci in range(HALF):
-                        c = h * HALF + ci
-                        cols = slice((k * HALF + ci) * P, (k * HALF + ci + 1) * P)
-                        nc.tensor.matmul_mx(
-                            out=acc[rs[k]][:],
-                            lhsT=codes[:, cols].bitcast(E4M3X4),
-                            lhsT_scale=scales[:, cols],
-                            rhs=g_codes[:, c, :].bitcast(E5M2X4),
-                            rhs_scale=g_scales[:, c, :],
-                            start=(c == 0),
-                            stop=(c == PASSES - 1),
-                        )
+                t[key] = four_bufs.tile([P, W], U32, name="codes", align_bytes=64)
+                t["scales_" + which] = four_bufs.tile([P, W], U8, name="scales", align_bytes=64)
+            words = slice(first * W // 4, (first + count) * W // 4)
+            nc.vector.quantize_mx(
+                out=t[key][:, words].bitcast(E4M3X4),
+                scales=t["scales_" + which][:, words],
+                in_=t[which][:, first : first + count, :].rearrange("p r n -> p (r n)"),
+            )
 
         RS_A = (7, 6, 0, 1)
         RS_B = (5, 4, 2, 3)
@@ -264,32 +280,44 @@ def tile_bsplinekanlayer_kernel(tc, x, coeff, base_weight, knots, grad_out, out)
             prepare_g(c)
         for t in range(UNITS):
             final = t == UNITS - 1
+            closing = t >= 3 and t % PER_BLOCK == 1
             if t + 2 < UNITS:
                 clip_and_sign(t + 2)
             relus(t)
+            add_function_5(t)
             if t >= 1:
                 mirror_on_scalar(t - 1)
+            if closing:
+                empty_banks((t - 3) // PER_BLOCK, RS_A + RS_B[0:2], "s")
+                multiply(t - 3, "four_b", RS_B, (2, 3))
+                multiply(t - 2, "four_b", RS_B, (2, 3))
             if t + 2 < UNITS:
                 squares(t + 2)
-            if t >= 3 and t % PER_BLOCK == 1:
-                empty_banks((t - 3) // PER_BLOCK, RS_A + RS_B, "s")
+            if closing:
+                empty_banks((t - 3) // PER_BLOCK, RS_B[2:4], "s")
             if t >= 4 and t % PER_BLOCK == 0:
                 weave_and_store((t - 4) // PER_BLOCK, "s", 2)
             if t + 1 < UNITS:
                 cubes(t + 1)
             combine_a(t, final)
             if t >= 1:
-                quantise_and_multiply(t - 1, "four_a", RS_A, ((0, 4),))
-                quantise_and_multiply(t - 1, "four_b", RS_B, ((0, 4),))
+                quantise(t - 1, "four_a", 0, 4)
+                multiply(t - 1, "four_a", RS_A, (0, 1, 2, 3))
+                quantise(t - 1, "four_b", 0, 4)
+                multiply(t - 1, "four_b", RS_B, (0, 1))
             if final:
-                quantise_and_multiply(t, "four_a", RS_A, ((0, 4),))
+                quantise(t, "four_a", 0, 4)
+                multiply(t, "four_a", RS_A, (0, 1, 2, 3))
                 weave_and_store(BLOCKS - 2, "s", 2)
                 empty_banks(BLOCKS - 1, RS_A, "s")
+                multiply(t - 1, "four_b", RS_B, (2, 3))
             combine_b(t)
             if final:
-                quantise_and_multiply(t, "four_b", RS_B, ((0, 2),))
+                quantise(t, "four_b", 0, 2)
+                multiply(t, "four_b", RS_B, (0, 1))
             combine_c(t, final)
             if final:
-                quantise_and_multiply(t, "four_b", RS_B, ((2, 2),))
+                quantise(t, "four_b", 2, 2)
+                multiply(t, "four_b", RS_B, (2, 3))
                 empty_banks(BLOCKS - 1, RS_B, "sv")
                 weave_and_store(BLOCKS - 1, "vs", 4)

@@ -76,11 +76,12 @@ def tile_bsplinekanlayer_kernel(tc, x, coeff, base_weight, knots, grad_out, out)
         g_scales = keep.tile([P, PASSES, NO], U8, align_bytes=64)
         g_raw = keep.tile([P, PASSES, PACK, NO], BF16, tag="planes", align_bytes=64)
         g_grp = keep.tile([P, PASSES, NO, PACK], BF16, tag="woven", align_bytes=64)
-        for c in range(PASSES):
-            nc.sync.dma_start(
-                out=x_raw[:, c],
-                in_=x[c * P * PACK : (c + 1) * P * PACK, :].rearrange("(p j) i -> p j i", j=PACK),
-            )
+        for cols in (slice(0, P), slice(P, NI)):
+            for c in range(PASSES):
+                nc.sync.dma_start(
+                    out=x_raw[:, c, :, cols],
+                    in_=x[c * P * PACK : (c + 1) * P * PACK, cols].rearrange("(p j) i -> p j i", j=PACK),
+                )
         for c in range(PASSES):
             nc.sync.dma_start(
                 out=g_raw[:, c],
@@ -142,16 +143,15 @@ def tile_bsplinekanlayer_kernel(tc, x, coeff, base_weight, knots, grad_out, out)
 
         def relus(u):
             t = tiles[u]
-            t["f_out"] = two.tile([P, 2, W], BF16, name="f_out")
-            t["f_lo"] = two.tile([P, 2, W], BF16, name="f_lo")
+            t["f"] = two.tile([P, 5, W], BF16, name="f")
             for name in ("u7", "u6", "w6", "w7"):
                 t[name] = upool.tile([P, W], F32, name="u")
             nc.scalar.activation(out=t["u7"][:], in_=t["y7"][:], func=ACT.Relu, scale=c2(7, 0))
-            nc.scalar.activation(out=t["f_out"][:, 0, :], in_=t["y7"][:], func=ACT.Relu, scale=c2(7, 0))
             nc.scalar.activation(out=t["u6"][:], in_=t["y6"][:], func=ACT.Relu, scale=c2(6, 0))
             nc.scalar.activation(out=t["w6"][:], in_=t["y6"][:], func=ACT.Relu, scale=-c2(2, 4))
-            nc.scalar.mul(out=t["f_lo"][:, 0, :], in_=t["w6"][:], mul=-1.0)
             nc.scalar.activation(out=t["w7"][:], in_=t["y7"][:], func=ACT.Relu, scale=-c2(3, 4))
+            nc.scalar.activation(out=t["f"][:, 0, :], in_=t["y7"][:], func=ACT.Relu, scale=c2(7, 0))
+            nc.scalar.mul(out=t["f"][:, 3, :], in_=t["w6"][:], mul=-1.0)
 
         def add_function_5(u):
             t = tiles[u]
@@ -167,47 +167,42 @@ def tile_bsplinekanlayer_kernel(tc, x, coeff, base_weight, knots, grad_out, out)
             t = tiles[u]
             t["t4"] = two.tile([P, W], F32, name="t4")
             axpy(t["t4"][:], t["w6"], c2(4, 2) / c2(2, 4), t["y8"], ALU.subtract)
-            axpy(t["f_out"][:, 1, :], t["u7"], c2(6, 1) / c2(7, 0), t["u6"], ALU.add)
-            s2 = t["s"][:].unsqueeze(1).to_broadcast([P, 2, W])
-            t["p_out"] = two.tile([P, 2, W], BF16, name="p_out")
-            nc.vector.tensor_tensor(out=t["p_out"][:], in0=t["f_out"][:], in1=s2, op=ALU.mult)
+            axpy(t["f"][:, 1, :], t["u7"], c2(6, 1) / c2(7, 0), t["u6"], ALU.add)
+            axpy(t["f"][:, 2, :], t["w6"], -c2(3, 3) / c2(2, 4), t["w7"], ALU.subtract)
+            axpy(t["f"][:, 4, :], t["w7"], c2(4, 3) / c2(3, 4), t["t4"], ALU.add)
+            t["p"] = two.tile([P, 6, W], BF16, name="p")
+            nc.vector.tensor_tensor(
+                out=t["p"][:, 0:5, :], in0=t["f"][:], in1=t["s"][:].unsqueeze(1).to_broadcast([P, 5, W]), op=ALU.mult
+            )
             t["four_a"] = three.tile([P, 4, W], BF16, name="four", align_bytes=64)
             nc.vector.tensor_scalar(
-                out=t["four_a"][:, 0:2, :], in0=t["p_out"][:], scalar1=0.0, scalar2=None, op0=ALU.max
+                out=t["four_a"][:, 0:2, :], in0=t["p"][:, 0:2, :], scalar1=0.0, scalar2=None, op0=ALU.max
             )
             if all_on_vector:
                 nc.vector.tensor_scalar(
-                    out=t["four_a"][:, 2:4, :], in0=t["p_out"][:], scalar1=-1.0, scalar2=0.0, op0=ALU.mult, op1=ALU.max
+                    out=t["four_a"][:, 2:4, :],
+                    in0=t["p"][:, 0:2, :],
+                    scalar1=-1.0,
+                    scalar2=0.0,
+                    op0=ALU.mult,
+                    op1=ALU.max,
                 )
 
         def combine_b(u):
             t = tiles[u]
-            t["f4"] = keep.tile([P, W], BF16, name="f4")
-            axpy(t["f4"][:], t["w7"], c2(4, 3) / c2(3, 4), t["t4"], ALU.add)
-            axpy(t["f_lo"][:, 1, :], t["w6"], -c2(3, 3) / c2(2, 4), t["w7"], ALU.subtract)
-            s2 = t["s"][:].unsqueeze(1).to_broadcast([P, 2, W])
-            t["p_hi"] = keep.tile([P, 2, W], BF16, name="p_hi")
             for n in range(W // NO):
                 cols = slice(n * NO, (n + 1) * NO)
-                nc.vector.tensor_tensor(out=t["p_hi"][:, 0, cols], in0=t["sum5"][n][:], in1=t["s"][:, cols], op=ALU.mult)
-            nc.vector.tensor_tensor(out=t["p_hi"][:, 1, :], in0=t["f4"][:], in1=t["s"][:], op=ALU.mult)
-            t["n_lo"] = two.tile([P, 2, W], BF16, name="n_lo")
-            nc.vector.tensor_tensor(out=t["n_lo"][:], in0=t["f_lo"][:], in1=s2, op=ALU.mult)
+                nc.vector.tensor_tensor(out=t["p"][:, 5, cols], in0=t["sum5"][n][:], in1=t["s"][:, cols], op=ALU.mult)
             t["four_b"] = three.tile([P, 4, W], BF16, name="four", align_bytes=64)
-            nc.vector.tensor_tensor(out=t["four_b"][:, 0:2, :], in0=t["p_hi"][:], in1=t["n_lo"][:], op=ALU.max)
+            nc.vector.tensor_tensor(out=t["four_b"][:, 0:2, :], in0=t["p"][:, 4:6, :], in1=t["p"][:, 2:4, :], op=ALU.max)
 
-        def combine_c(u, all_on_vector):
+        def combine_c(u):
             t = tiles[u]
-            nc.vector.tensor_tensor(out=t["n_lo"][:], in0=t["p_hi"][:], in1=t["n_lo"][:], op=ALU.min)
-            if all_on_vector:
-                nc.vector.tensor_scalar(
-                    out=t["four_b"][:, 2:4, :], in0=t["n_lo"][:], scalar1=-1.0, scalar2=None, op0=ALU.mult
-                )
+            nc.vector.tensor_tensor(out=t["four_b"][:, 2:4, :], in0=t["p"][:, 4:6, :], in1=t["p"][:, 2:4, :], op=ALU.min)
 
         def mirror_on_scalar(u):
             t = tiles[u]
-            nc.scalar.activation(out=t["four_a"][:, 2:4, :], in_=t["p_out"][:], func=ACT.Relu, scale=-1.0)
-            nc.scalar.mul(out=t["four_b"][:, 2:4, :], in_=t["n_lo"][:], mul=-1.0)
+            nc.scalar.activation(out=t["four_a"][:, 2:4, :], in_=t["p"][:, 0:2, :], func=ACT.Relu, scale=-1.0)
 
         def multiply(u, which, rs, ks):
             t = tiles[u]
@@ -242,15 +237,19 @@ def tile_bsplinekanlayer_kernel(tc, x, coeff, base_weight, knots, grad_out, out)
             )
 
         RS_A = (7, 6, 0, 1)
-        RS_B = (5, 4, 2, 3)
+        RS_B = (4, 5, 3, 2)
+        NEGATED = (3, 2)
         planes = {}
 
         def empty_banks(b, rs, engines):
             if b not in planes:
                 planes[b] = keep.tile([P, NB, NO], F32, tag="planes", name="planes", align_bytes=64)
             for n, r in enumerate(rs):
+                sign = -1.0 if r in NEGATED else 1.0
                 if engines[n % len(engines)] == "v":
-                    nc.vector.tensor_copy(out=planes[b][:, r, :], in_=acc[r][:])
+                    nc.vector.tensor_scalar(out=planes[b][:, r, :], in0=acc[r][:], scalar1=sign, scalar2=None, op0=ALU.mult)
+                elif r in NEGATED:
+                    nc.scalar.mul(out=planes[b][:, r, :], in_=acc[r][:], mul=sign)
                 else:
                     nc.scalar.copy(out=planes[b][:, r, :], in_=acc[r][:])
 
@@ -315,7 +314,7 @@ def tile_bsplinekanlayer_kernel(tc, x, coeff, base_weight, knots, grad_out, out)
             if final:
                 quantise(t, "four_b", 0, 2)
                 multiply(t, "four_b", RS_B, (0, 1))
-            combine_c(t, final)
+            combine_c(t)
             if final:
                 quantise(t, "four_b", 2, 2)
                 multiply(t, "four_b", RS_B, (2, 3))

@@ -175,9 +175,10 @@ def tile_bsplinekanlayer_kernel(tc, x, coeff, base_weight, knots, grad_out, out)
                 out=t["p"][:, 0:5, :], in0=t["f"][:], in1=t["s"][:].unsqueeze(1).to_broadcast([P, 5, W]), op=ALU.mult
             )
             t["four_a"] = three.tile([P, 4, W], BF16, name="four", align_bytes=64)
-            nc.vector.tensor_scalar(
-                out=t["four_a"][:, 0:2, :], in0=t["p"][:, 0:2, :], scalar1=0.0, scalar2=None, op0=ALU.max
-            )
+            if all_on_vector:
+                nc.vector.tensor_scalar(
+                    out=t["four_a"][:, 0:2, :], in0=t["p"][:, 0:2, :], scalar1=0.0, scalar2=None, op0=ALU.max
+                )
             if all_on_vector:
                 nc.vector.tensor_scalar(
                     out=t["four_a"][:, 2:4, :],
@@ -203,6 +204,7 @@ def tile_bsplinekanlayer_kernel(tc, x, coeff, base_weight, knots, grad_out, out)
         def mirror_on_scalar(u):
             t = tiles[u]
             nc.scalar.activation(out=t["four_a"][:, 2:4, :], in_=t["p"][:, 0:2, :], func=ACT.Relu, scale=-1.0)
+            nc.scalar.activation(out=t["four_a"][:, 0:2, :], in_=t["p"][:, 0:2, :], func=ACT.Relu)
 
         def multiply(u, which, rs, ks):
             t = tiles[u]

@@ -93,8 +93,10 @@ def tile_bsplinekanlayer_kernel(tc, x, coeff, base_weight, knots, grad_out, out)
         nc.scalar.mul(out=diag[1][:], in_=diag[0][:], mul=c2(5, 1) / c2(6, 0))
         nc.scalar.mul(out=diag[2][:], in_=diag[0][:], mul=c2(5, 2) / c2(7, 0))
 
-        def prepare_g(c):
+        def regroup_g(c):
             nc.vector.tensor_copy(out=g_grp[:, c], in_=g_raw[:, c].rearrange("p j o -> p o j"))
+
+        def quantise_g(c):
             nc.vector.quantize_mx(
                 out=g_codes[:, c, :].bitcast(E5M2X4),
                 scales=g_scales[:, c, :],
@@ -108,7 +110,7 @@ def tile_bsplinekanlayer_kernel(tc, x, coeff, base_weight, knots, grad_out, out)
         def axpy(dst, a, factor, b, op1):
             nc.vector.scalar_tensor_tensor(out=dst, in0=a[:], scalar=factor, in1=b[:], op0=ALU.mult, op1=op1)
 
-        def clip_and_sign(u):
+        def clip(u):
             t = tiles[u]
             b = u // PER_BLOCK
             h = u % PER_BLOCK
@@ -121,15 +123,21 @@ def tile_bsplinekanlayer_kernel(tc, x, coeff, base_weight, knots, grad_out, out)
                 op0=ALU.max,
                 op1=ALU.min,
             )
+
+        def sign(u):
+            t = tiles[u]
             t["s"] = three.tile([P, W], BF16, name="s")
             nc.vector.tensor_scalar(
                 out=t["s"][:], in0=t["xc"][:], scalar1=0.0, scalar2=0.5, op0=ALU.is_ge, op1=ALU.subtract
             )
 
-        def squares(u):
+        def absolute(u):
             t = tiles[u]
             t["z"] = two.tile([P, W], BF16, name="z")
             nc.scalar.activation(out=t["z"][:], in_=t["xc"][:], func=ACT.Abs)
+
+        def squares(u):
+            t = tiles[u]
             for name, shift, scale in CUBES:
                 t[name] = two.tile([P, W], F32, name=name)
                 nc.scalar.activation(out=t[name][:], in_=t["z"][:], func=ACT.Square, bias=scale * shift, scale=scale)
@@ -163,13 +171,16 @@ def tile_bsplinekanlayer_kernel(tc, x, coeff, base_weight, knots, grad_out, out)
                     nc.tensor.matmul(out=bank[:], lhsT=diag[k][:], rhs=t[name][:, cols], start=(k == 0), stop=(k == 2))
                 t["sum5"].append(bank)
 
-        def combine_a(u, all_on_vector):
+        def combine_a(u):
             t = tiles[u]
             t["t4"] = two.tile([P, W], F32, name="t4")
             axpy(t["t4"][:], t["w6"], c2(4, 2) / c2(2, 4), t["y8"], ALU.subtract)
             axpy(t["f"][:, 1, :], t["u7"], c2(6, 1) / c2(7, 0), t["u6"], ALU.add)
             axpy(t["f"][:, 2, :], t["w6"], -c2(3, 3) / c2(2, 4), t["w7"], ALU.subtract)
             axpy(t["f"][:, 4, :], t["w7"], c2(4, 3) / c2(3, 4), t["t4"], ALU.add)
+
+        def times_sign(u, all_on_vector):
+            t = tiles[u]
             t["p"] = two.tile([P, 6, W], BF16, name="p")
             nc.vector.tensor_tensor(
                 out=t["p"][:, 0:5, :], in0=t["f"][:], in1=t["s"][:].unsqueeze(1).to_broadcast([P, 5, W]), op=ALU.mult
@@ -194,6 +205,9 @@ def tile_bsplinekanlayer_kernel(tc, x, coeff, base_weight, knots, grad_out, out)
             for n in range(W // NO):
                 cols = slice(n * NO, (n + 1) * NO)
                 nc.vector.tensor_tensor(out=t["p"][:, 5, cols], in0=t["sum5"][n][:], in1=t["s"][:, cols], op=ALU.mult)
+
+        def combine_b2(u):
+            t = tiles[u]
             t["four_b"] = three.tile([P, 4, W], BF16, name="four", align_bytes=64)
             nc.vector.tensor_tensor(out=t["four_b"][:, 0:2, :], in0=t["p"][:, 4:6, :], in1=t["p"][:, 2:4, :], op=ALU.max)
 
@@ -272,20 +286,30 @@ def tile_bsplinekanlayer_kernel(tc, x, coeff, base_weight, knots, grad_out, out)
                     o_st = slice((oq + 1 - step) * quarter, (oq + 1) * quarter)
                     nc.sync.dma_start(out=out[b * P : (b + 1) * P, o_st, :], in_=woven[:, o_st, :])
 
-        clip_and_sign(0)
-        clip_and_sign(1)
+        clip(0)
+        clip(1)
+        sign(0)
+        sign(1)
+        absolute(0)
+        absolute(1)
         squares(0)
         squares(1)
         cubes(0)
-        for c in range(PASSES):
-            prepare_g(c)
+        regroup_g(0)
+        for c in range(1, PASSES):
+            regroup_g(c)
+            quantise_g(c - 1)
         for t in range(UNITS):
             final = t == UNITS - 1
             closing = t >= 3 and t % PER_BLOCK == 1
             if t + 2 < UNITS:
-                clip_and_sign(t + 2)
+                clip(t + 2)
+            if t == 0:
+                quantise_g(PASSES - 1)
             relus(t)
             add_function_5(t)
+            if t + 2 < UNITS:
+                absolute(t + 2)
             if t >= 1:
                 mirror_on_scalar(t - 1)
             if closing:
@@ -300,11 +324,13 @@ def tile_bsplinekanlayer_kernel(tc, x, coeff, base_weight, knots, grad_out, out)
                 weave_and_store((t - 4) // PER_BLOCK, "s", 2)
             if t + 1 < UNITS:
                 cubes(t + 1)
-            combine_a(t, final)
+            combine_a(t)
+            if t >= 1:
+                quantise(t - 1, "four_b", 0, 4)
+            times_sign(t, final)
             if t >= 1:
                 quantise(t - 1, "four_a", 0, 4)
                 multiply(t - 1, "four_a", RS_A, (0, 1, 2, 3))
-                quantise(t - 1, "four_b", 0, 4)
                 multiply(t - 1, "four_b", RS_B, (0, 1))
             if final:
                 quantise(t, "four_a", 0, 4)
@@ -313,6 +339,9 @@ def tile_bsplinekanlayer_kernel(tc, x, coeff, base_weight, knots, grad_out, out)
                 empty_banks(BLOCKS - 1, RS_A, "s")
                 multiply(t - 1, "four_b", RS_B, (2, 3))
             combine_b(t)
+            if t + 2 < UNITS:
+                sign(t + 2)
+            combine_b2(t)
             if final:
                 quantise(t, "four_b", 0, 2)
                 multiply(t, "four_b", RS_B, (0, 1))

@@ -142,9 +142,9 @@ def tile_bsplinekanlayer_kernel(tc, x, coeff, base_weight, knots, grad_out, out)
                 t[name] = two.tile([P, W], F32, name=name)
                 nc.scalar.activation(out=t[name][:], in_=t["z"][:], func=ACT.Square, bias=scale * shift, scale=scale)
 
-        def cubes(u):
+        def cubes(u, first, count):
             t = tiles[u]
-            for name, shift, scale in CUBES:
+            for name, shift, scale in CUBES[first : first + count]:
                 nc.vector.scalar_tensor_tensor(
                     out=t[name][:], in0=t["z"][:], scalar=shift, in1=t[name][:], op0=ALU.add, op1=ALU.mult
                 )
@@ -291,25 +291,21 @@ def tile_bsplinekanlayer_kernel(tc, x, coeff, base_weight, knots, grad_out, out)
         sign(0)
         sign(1)
         absolute(0)
-        absolute(1)
         squares(0)
+        absolute(1)
         squares(1)
-        cubes(0)
-        regroup_g(0)
-        for c in range(1, PASSES):
+        cubes(0, 0, 4)
+        for c in range(PASSES):
             regroup_g(c)
-            quantise_g(c - 1)
+        for c in range(PASSES):
+            quantise_g(c)
         for t in range(UNITS):
             final = t == UNITS - 1
             closing = t >= 3 and t % PER_BLOCK == 1
             if t + 2 < UNITS:
                 clip(t + 2)
-            if t == 0:
-                quantise_g(PASSES - 1)
             relus(t)
             add_function_5(t)
-            if t + 2 < UNITS:
-                absolute(t + 2)
             if t >= 1:
                 mirror_on_scalar(t - 1)
             if closing:
@@ -317,20 +313,28 @@ def tile_bsplinekanlayer_kernel(tc, x, coeff, base_weight, knots, grad_out, out)
                 multiply(t - 3, "four_b", RS_B, (2, 3))
                 multiply(t - 2, "four_b", RS_B, (2, 3))
             if t + 2 < UNITS:
+                absolute(t + 2)
                 squares(t + 2)
             if closing:
                 empty_banks((t - 3) // PER_BLOCK, RS_B[2:4], "s")
             if t >= 4 and t % PER_BLOCK == 0:
                 weave_and_store((t - 4) // PER_BLOCK, "s", 2)
             if t + 1 < UNITS:
-                cubes(t + 1)
+                cubes(t + 1, 0, 2)
+            if t + 2 < UNITS:
+                sign(t + 2)
+            if t + 1 < UNITS:
+                cubes(t + 1, 2, 1)
             combine_a(t)
-            if t >= 1:
-                quantise(t - 1, "four_b", 0, 4)
+            if t + 1 < UNITS:
+                cubes(t + 1, 3, 1)
             times_sign(t, final)
+            if not final:
+                combine_b(t)
             if t >= 1:
                 quantise(t - 1, "four_a", 0, 4)
                 multiply(t - 1, "four_a", RS_A, (0, 1, 2, 3))
+                quantise(t - 1, "four_b", 0, 4)
                 multiply(t - 1, "four_b", RS_B, (0, 1))
             if final:
                 quantise(t, "four_a", 0, 4)
@@ -338,9 +342,7 @@ def tile_bsplinekanlayer_kernel(tc, x, coeff, base_weight, knots, grad_out, out)
                 weave_and_store(BLOCKS - 2, "s", 2)
                 empty_banks(BLOCKS - 1, RS_A, "s")
                 multiply(t - 1, "four_b", RS_B, (2, 3))
-            combine_b(t)
-            if t + 2 < UNITS:
-                sign(t + 2)
+                combine_b(t)
             combine_b2(t)
             if final:
                 quantise(t, "four_b", 0, 2)

@@ -215,10 +215,20 @@ def tile_bsplinekanlayer_kernel(tc, x, coeff, base_weight, knots, grad_out, out)
             t = tiles[u]
             nc.vector.tensor_tensor(out=t["four_b"][:, 2:4, :], in0=t["p"][:, 4:6, :], in1=t["p"][:, 2:4, :], op=ALU.min)
 
+        def plus_on_vector(u):
+            return u % 2 == 1
+
         def mirror_on_scalar(u):
             t = tiles[u]
             nc.scalar.activation(out=t["four_a"][:, 2:4, :], in_=t["p"][:, 0:2, :], func=ACT.Relu, scale=-1.0)
-            nc.scalar.activation(out=t["four_a"][:, 0:2, :], in_=t["p"][:, 0:2, :], func=ACT.Relu)
+            if not plus_on_vector(u):
+                nc.scalar.activation(out=t["four_a"][:, 0:2, :], in_=t["p"][:, 0:2, :], func=ACT.Relu)
+
+        def mirror_on_vector(u):
+            t = tiles[u]
+            nc.vector.tensor_scalar(
+                out=t["four_a"][:, 0:2, :], in0=t["p"][:, 0:2, :], scalar1=0.0, scalar2=None, op0=ALU.max
+            )
 
         def multiply(u, which, rs, ks):
             t = tiles[u]
@@ -331,6 +341,8 @@ def tile_bsplinekanlayer_kernel(tc, x, coeff, base_weight, knots, grad_out, out)
             times_sign(t, final)
             if not final:
                 combine_b(t)
+                if plus_on_vector(t):
+                    mirror_on_vector(t)
             if t >= 1:
                 quantise(t - 1, "four_a", 0, 4)
                 multiply(t - 1, "four_a", RS_A, (0, 1, 2, 3))

@@ -216,7 +216,7 @@ def tile_bsplinekanlayer_kernel(tc, x, coeff, base_weight, knots, grad_out, out)
             nc.vector.tensor_tensor(out=t["four_b"][:, 2:4, :], in0=t["p"][:, 4:6, :], in1=t["p"][:, 2:4, :], op=ALU.min)
 
         def plus_on_vector(u):
-            return u % 2 == 1
+            return True
 
         def mirror_on_scalar(u):
             t = tiles[u]

@@ -151,7 +151,7 @@ def tile_bsplinekanlayer_kernel(tc, x, coeff, base_weight, knots, grad_out, out)
 
         def relus(u):
             t = tiles[u]
-            t["f"] = two.tile([P, 5, W], BF16, name="f")
+            t["f"] = two.tile([P, 6, W], BF16, name="f")
             for name in ("u7", "u6", "w6", "w7"):
                 t[name] = upool.tile([P, W], F32, name="u")
             nc.scalar.activation(out=t["u7"][:], in_=t["y7"][:], func=ACT.Relu, scale=c2(7, 0))
@@ -183,7 +183,7 @@ def tile_bsplinekanlayer_kernel(tc, x, coeff, base_weight, knots, grad_out, out)
             t = tiles[u]
             t["p"] = two.tile([P, 6, W], BF16, name="p")
             nc.vector.tensor_tensor(
-                out=t["p"][:, 0:5, :], in0=t["f"][:], in1=t["s"][:].unsqueeze(1).to_broadcast([P, 5, W]), op=ALU.mult
+                out=t["p"][:, 0:5, :], in0=t["f"][:, 0:5, :], in1=t["s"][:].unsqueeze(1).to_broadcast([P, 5, W]), op=ALU.mult
             )
             t["four_a"] = three.tile([P, 4, W], BF16, name="four", align_bytes=64)
             if all_on_vector:
@@ -200,11 +200,14 @@ def tile_bsplinekanlayer_kernel(tc, x, coeff, base_weight, knots, grad_out, out)
                     op1=ALU.max,
                 )
 
-        def combine_b(u):
+        def round_function_5(u):
             t = tiles[u]
             for n in range(W // NO):
-                cols = slice(n * NO, (n + 1) * NO)
-                nc.vector.tensor_tensor(out=t["p"][:, 5, cols], in0=t["sum5"][n][:], in1=t["s"][:, cols], op=ALU.mult)
+                nc.scalar.copy(out=t["f"][:, 5, n * NO : (n + 1) * NO], in_=t["sum5"][n][:])
+
+        def combine_b(u):
+            t = tiles[u]
+            nc.vector.tensor_tensor(out=t["p"][:, 5, :], in0=t["f"][:, 5, :], in1=t["s"][:], op=ALU.mult)
 
         def combine_b2(u):
             t = tiles[u]
@@ -312,8 +315,13 @@ def tile_bsplinekanlayer_kernel(tc, x, coeff, base_weight, knots, grad_out, out)
         for t in range(UNITS):
             final = t == UNITS - 1
             closing = t >= 3 and t % PER_BLOCK == 1
+            if t >= 1:
+                combine_b(t - 1)
             if t + 2 < UNITS:
                 clip(t + 2)
+            if t >= 1:
+                combine_b2(t - 1)
+                combine_c(t - 1)
             relus(t)
             add_function_5(t)
             if t >= 1:
@@ -325,6 +333,7 @@ def tile_bsplinekanlayer_kernel(tc, x, coeff, base_weight, knots, grad_out, out)
             if t + 2 < UNITS:
                 absolute(t + 2)
                 squares(t + 2)
+            round_function_5(t)
             if closing:
                 empty_banks((t - 3) // PER_BLOCK, RS_B[2:4], "s")
             if t >= 4 and t % PER_BLOCK == 0:
@@ -339,15 +348,13 @@ def tile_bsplinekanlayer_kernel(tc, x, coeff, base_weight, knots, grad_out, out)
             if t + 1 < UNITS:
                 cubes(t + 1, 3, 1)
             times_sign(t, final)
-            if not final:
-                combine_b(t)
-                if plus_on_vector(t):
-                    mirror_on_vector(t)
             if t >= 1:
                 quantise(t - 1, "four_a", 0, 4)
                 multiply(t - 1, "four_a", RS_A, (0, 1, 2, 3))
                 quantise(t - 1, "four_b", 0, 4)
                 multiply(t - 1, "four_b", RS_B, (0, 1))
+            if not final:
+                mirror_on_vector(t)
             if final:
                 quantise(t, "four_a", 0, 4)
                 multiply(t, "four_a", RS_A, (0, 1, 2, 3))
@@ -355,12 +362,10 @@ def tile_bsplinekanlayer_kernel(tc, x, coeff, base_weight, knots, grad_out, out)
                 empty_banks(BLOCKS - 1, RS_A, "s")
                 multiply(t - 1, "four_b", RS_B, (2, 3))
                 combine_b(t)
-            combine_b2(t)
-            if final:
+                combine_b2(t)
                 quantise(t, "four_b", 0, 2)
                 multiply(t, "four_b", RS_B, (0, 1))
-            combine_c(t)
-            if final:
+                combine_c(t)
                 quantise(t, "four_b", 2, 2)
                 multiply(t, "four_b", RS_B, (2, 3))
                 empty_banks(BLOCKS - 1, RS_B, "sv")

@@ -218,19 +218,26 @@ def tile_bsplinekanlayer_kernel(tc, x, coeff, base_weight, knots, grad_out, out)
             t = tiles[u]
             nc.vector.tensor_tensor(out=t["four_b"][:, 2:4, :], in0=t["p"][:, 4:6, :], in1=t["p"][:, 2:4, :], op=ALU.min)
 
-        def plus_on_vector(u):
-            return True
+        def scalar_has_room(step):
+            return (step < 3 or step + 2 >= UNITS) and step != UNITS - 1
 
         def mirror_on_scalar(u):
             t = tiles[u]
             nc.scalar.activation(out=t["four_a"][:, 2:4, :], in_=t["p"][:, 0:2, :], func=ACT.Relu, scale=-1.0)
-            if not plus_on_vector(u):
-                nc.scalar.activation(out=t["four_a"][:, 0:2, :], in_=t["p"][:, 0:2, :], func=ACT.Relu)
+            nc.scalar.activation(out=t["four_a"][:, 0:2, :], in_=t["p"][:, 0:2, :], func=ACT.Relu)
 
         def mirror_on_vector(u):
             t = tiles[u]
             nc.vector.tensor_scalar(
                 out=t["four_a"][:, 0:2, :], in0=t["p"][:, 0:2, :], scalar1=0.0, scalar2=None, op0=ALU.max
+            )
+            nc.vector.tensor_scalar(
+                out=t["four_a"][:, 2:4, :],
+                in0=t["p"][:, 0:2, :],
+                scalar1=-1.0,
+                scalar2=0.0,
+                op0=ALU.mult,
+                op1=ALU.max,
             )
 
         def multiply(u, which, rs, ks):
@@ -324,7 +331,7 @@ def tile_bsplinekanlayer_kernel(tc, x, coeff, base_weight, knots, grad_out, out)
                 combine_c(t - 1)
             relus(t)
             add_function_5(t)
-            if t >= 1:
+            if t >= 1 and scalar_has_room(t):
                 mirror_on_scalar(t - 1)
             if closing:
                 empty_banks((t - 3) // PER_BLOCK, RS_A + RS_B[0:2], "s")
@@ -353,7 +360,7 @@ def tile_bsplinekanlayer_kernel(tc, x, coeff, base_weight, knots, grad_out, out)
                 multiply(t - 1, "four_a", RS_A, (0, 1, 2, 3))
                 quantise(t - 1, "four_b", 0, 4)
                 multiply(t - 1, "four_b", RS_B, (0, 1))
-            if not final:
+            if not final and not scalar_has_room(t + 1):
                 mirror_on_vector(t)
             if final:
                 quantise(t, "four_a", 0, 4)

@@ -66,7 +66,7 @@ def tile_bsplinekanlayer_kernel(tc, x, coeff, base_weight, knots, grad_out, out)
         keep = ctx.enter_context(tc.tile_pool(name="keep", bufs=1))
         two = ctx.enter_context(tc.tile_pool(name="two", bufs=2))
         three = ctx.enter_context(tc.tile_pool(name="three", bufs=3))
-        upool = ctx.enter_context(tc.tile_pool(name="upool", bufs=6))
+        upool = ctx.enter_context(tc.tile_pool(name="upool", bufs=3))
         four_bufs = ctx.enter_context(tc.tile_pool(name="four_bufs", bufs=4))
         psum = ctx.enter_context(tc.psum_pool(name="psum", bufs=6))
         psum_sum = ctx.enter_context(tc.psum_pool(name="psum_sum", bufs=2))
@@ -91,7 +91,7 @@ def tile_bsplinekanlayer_kernel(tc, x, coeff, base_weight, knots, grad_out, out)
         diag = [keep.tile([P, P], F32, name="diag%d" % n) for n in range(3)]
         make_identity(nc, diag[0][:])
         nc.scalar.mul(out=diag[1][:], in_=diag[0][:], mul=c2(5, 1) / c2(6, 0))
-        nc.scalar.mul(out=diag[2][:], in_=diag[0][:], mul=c2(5, 2) / c2(7, 0))
+        nc.scalar.mul(out=diag[2][:], in_=diag[0][:], mul=c2(5, 2) / c2(6, 0))
 
         def regroup_g(c):
             nc.vector.tensor_copy(out=g_grp[:, c], in_=g_raw[:, c].rearrange("p j o -> p o j"))
@@ -108,7 +108,7 @@ def tile_bsplinekanlayer_kernel(tc, x, coeff, base_weight, knots, grad_out, out)
         CUBES = (("y7", -t7, 1.0), ("y6", -t6, 1.0), ("y5", t6, math.sqrt(c2(5, 0))), ("y8", -1.0, math.sqrt(c2(4, 4))))
 
         def axpy(dst, a, factor, b, op1):
-            nc.vector.scalar_tensor_tensor(out=dst, in0=a[:], scalar=factor, in1=b[:], op0=ALU.mult, op1=op1)
+            nc.vector.scalar_tensor_tensor(out=dst, in0=a, scalar=factor, in1=b, op0=ALU.mult, op1=op1)
 
         def clip(u):
             t = tiles[u]
@@ -138,28 +138,37 @@ def tile_bsplinekanlayer_kernel(tc, x, coeff, base_weight, knots, grad_out, out)
 
         def squares(u):
             t = tiles[u]
+            y76 = two.tile([P, 2, W], F32, name="y76")
+            t["y76"] = y76
+            t["y7"] = y76[:, 0, :]
+            t["y6"] = y76[:, 1, :]
+            y5 = two.tile([P, W], F32, name="y5")
+            t["y5"] = y5[:]
+            y8 = two.tile([P, W], F32, name="y8")
+            t["y8"] = y8[:]
             for name, shift, scale in CUBES:
-                t[name] = two.tile([P, W], F32, name=name)
-                nc.scalar.activation(out=t[name][:], in_=t["z"][:], func=ACT.Square, bias=scale * shift, scale=scale)
+                nc.scalar.activation(out=t[name], in_=t["z"][:], func=ACT.Square, bias=scale * shift, scale=scale)
 
         def cubes(u, first, count):
             t = tiles[u]
             for name, shift, scale in CUBES[first : first + count]:
                 nc.vector.scalar_tensor_tensor(
-                    out=t[name][:], in0=t["z"][:], scalar=shift, in1=t[name][:], op0=ALU.add, op1=ALU.mult
+                    out=t[name], in0=t["z"][:], scalar=shift, in1=t[name], op0=ALU.add, op1=ALU.mult
                 )
 
         def relus(u):
             t = tiles[u]
             t["f"] = two.tile([P, 6, W], BF16, name="f")
-            for name in ("u7", "u6", "w6", "w7"):
-                t[name] = upool.tile([P, W], F32, name="u")
-            nc.scalar.activation(out=t["u7"][:], in_=t["y7"][:], func=ACT.Relu, scale=c2(7, 0))
-            nc.scalar.activation(out=t["u6"][:], in_=t["y6"][:], func=ACT.Relu, scale=c2(6, 0))
-            nc.scalar.activation(out=t["w6"][:], in_=t["y6"][:], func=ACT.Relu, scale=-c2(2, 4))
-            nc.scalar.activation(out=t["w7"][:], in_=t["y7"][:], func=ACT.Relu, scale=-c2(3, 4))
-            nc.scalar.activation(out=t["f"][:, 0, :], in_=t["y7"][:], func=ACT.Relu, scale=c2(7, 0))
-            nc.scalar.mul(out=t["f"][:, 3, :], in_=t["w6"][:], mul=-1.0)
+            rising = upool.tile([P, 2, W], F32, name="u")
+            falling = upool.tile([P, 2, W], F32, name="u")
+            t["u7"] = rising[:, 0, :]
+            t["u6"] = rising[:, 1, :]
+            t["w7"] = falling[:, 0, :]
+            t["w6"] = falling[:, 1, :]
+            nc.scalar.activation(out=rising[:], in_=t["y76"][:], func=ACT.Relu, scale=c2(6, 0))
+            nc.scalar.activation(out=falling[:], in_=t["y76"][:], func=ACT.Relu, scale=-c2(3, 4))
+            nc.scalar.activation(out=t["f"][:, 0, :], in_=t["y7"], func=ACT.Relu, scale=c2(7, 0))
+            nc.scalar.mul(out=t["f"][:, 3, :], in_=t["w6"], mul=-c2(2, 4) / c2(3, 4))
 
         def add_function_5(u):
             t = tiles[u]
@@ -173,11 +182,11 @@ def tile_bsplinekanlayer_kernel(tc, x, coeff, base_weight, knots, grad_out, out)
 
         def combine_a(u):
             t = tiles[u]
-            t["t4"] = two.tile([P, W], F32, name="t4")
-            axpy(t["t4"][:], t["w6"], c2(4, 2) / c2(2, 4), t["y8"], ALU.subtract)
-            axpy(t["f"][:, 1, :], t["u7"], c2(6, 1) / c2(7, 0), t["u6"], ALU.add)
-            axpy(t["f"][:, 2, :], t["w6"], -c2(3, 3) / c2(2, 4), t["w7"], ALU.subtract)
-            axpy(t["f"][:, 4, :], t["w7"], c2(4, 3) / c2(3, 4), t["t4"], ALU.add)
+            t4 = two.tile([P, W], F32, name="t4")
+            axpy(t4[:], t["w6"], c2(4, 2) / c2(3, 4), t["y8"], ALU.subtract)
+            axpy(t["f"][:, 1, :], t["u7"], c2(6, 1) / c2(6, 0), t["u6"], ALU.add)
+            axpy(t["f"][:, 2, :], t["w6"], -c2(3, 3) / c2(3, 4), t["w7"], ALU.subtract)
+            axpy(t["f"][:, 4, :], t["w7"], c2(4, 3) / c2(3, 4), t4[:], ALU.add)
 
         def times_sign(u, all_on_vector):
             t = tiles[u]
@@ -291,20 +300,17 @@ def tile_bsplinekanlayer_kernel(tc, x, coeff, base_weight, knots, grad_out, out)
 
         def weave_and_store(b, engines, stores):
             woven = keep.tile([P, NO, NB], F32, tag="woven", name="woven", align_bytes=64)
-            quarter = NO // 4
-            for oq in range(4):
-                o_cols = slice(oq * quarter, (oq + 1) * quarter)
+            piece = NO // stores
+            for n in range(stores):
+                o_cols = slice(n * piece, (n + 1) * piece)
                 for rq in range(2):
                     r_rows = slice(rq * 4, (rq + 1) * 4)
                     src = planes[b][:, r_rows, o_cols].rearrange("p r o -> p o r")
-                    if engines[oq % len(engines)] == "v":
+                    if engines[n % len(engines)] == "v":
                         nc.vector.tensor_copy(out=woven[:, o_cols, r_rows], in_=src)
                     else:
                         nc.scalar.copy(out=woven[:, o_cols, r_rows], in_=src)
-                step = 4 // stores
-                if (oq + 1) % step == 0:
-                    o_st = slice((oq + 1 - step) * quarter, (oq + 1) * quarter)
-                    nc.sync.dma_start(out=out[b * P : (b + 1) * P, o_st, :], in_=woven[:, o_st, :])
+                nc.sync.dma_start(out=out[b * P : (b + 1) * P, o_cols, :], in_=woven[:, o_cols, :])
 
         clip(0)
         clip(1)

@@ -71,22 +71,26 @@ def tile_bsplinekanlayer_kernel(tc, x, coeff, base_weight, knots, grad_out, out)
         psum = ctx.enter_context(tc.psum_pool(name="psum", bufs=6))
         psum_sum = ctx.enter_context(tc.psum_pool(name="psum_sum", bufs=2))
 
-        x_raw = keep.tile([P, PASSES, PACK, NI], BF16)
+        x_raw = keep.tile([P, PACK, NI // P, PASSES, P], BF16)
         g_codes = keep.tile([P, PASSES, NO], U32, align_bytes=64)
         g_scales = keep.tile([P, PASSES, NO], U8, align_bytes=64)
         g_raw = keep.tile([P, PASSES, PACK, NO], BF16, tag="planes", align_bytes=64)
         g_grp = keep.tile([P, PASSES, NO, PACK], BF16, tag="woven", align_bytes=64)
-        for cols in (slice(0, P), slice(P, NI)):
+        def load_x(b):
             for c in range(PASSES):
                 nc.sync.dma_start(
-                    out=x_raw[:, c, :, cols],
-                    in_=x[c * P * PACK : (c + 1) * P * PACK, cols].rearrange("(p j) i -> p j i", j=PACK),
+                    out=x_raw[:, :, b, c, :],
+                    in_=x[c * P * PACK : (c + 1) * P * PACK, b * P : (b + 1) * P].rearrange("(p j) i -> p j i", j=PACK),
                 )
+
+        load_x(0)
         for c in range(PASSES):
             nc.sync.dma_start(
                 out=g_raw[:, c],
                 in_=grad_out[c * P * PACK : (c + 1) * P * PACK, :].rearrange("(p j) o -> p j o", j=PACK),
             )
+        for b in range(1, NI // P):
+            load_x(b)
 
         diag = [keep.tile([P, P], F32, name="diag%d" % n) for n in range(3)]
         make_identity(nc, diag[0][:])
@@ -94,7 +98,9 @@ def tile_bsplinekanlayer_kernel(tc, x, coeff, base_weight, knots, grad_out, out)
         nc.scalar.mul(out=diag[2][:], in_=diag[0][:], mul=c2(5, 2) / c2(6, 0))
 
         def regroup_g(c):
-            nc.vector.tensor_copy(out=g_grp[:, c], in_=g_raw[:, c].rearrange("p j o -> p o j"))
+            nc.vector.tensor_copy(
+                out=g_grp[:, c].rearrange("p (q i) j -> p q j i", i=4), in_=g_raw[:, c].rearrange("p j (q i) -> p q j i", i=4)
+            )
 
         def quantise_g(c):
             nc.vector.quantize_mx(
@@ -116,8 +122,8 @@ def tile_bsplinekanlayer_kernel(tc, x, coeff, base_weight, knots, grad_out, out)
             h = u % PER_BLOCK
             t["xc"] = two.tile([P, W], BF16, name="xc")
             nc.vector.tensor_scalar(
-                out=t["xc"][:].rearrange("p (c i j) -> p c i j", c=HALF, i=P, j=PACK),
-                in0=x_raw[:, h * HALF : (h + 1) * HALF, :, b * P : (b + 1) * P].rearrange("p c j i -> p c i j"),
+                out=t["xc"][:].rearrange("p (q i j) -> p q j i", i=4, j=PACK),
+                in0=x_raw[:, :, b, h * HALF : (h + 1) * HALF, :].rearrange("p j c (q i) -> p (c q) j i", i=4),
                 scalar1=-1.0,
                 scalar2=1.0,
                 op0=ALU.max,

@@ -311,11 +311,12 @@ def tile_bsplinekanlayer_kernel(tc, x, coeff, base_weight, knots, grad_out, out)
                 o_cols = slice(n * piece, (n + 1) * piece)
                 for rq in range(2):
                     r_rows = slice(rq * 4, (rq + 1) * 4)
-                    src = planes[b][:, r_rows, o_cols].rearrange("p r o -> p o r")
+                    src = planes[b][:, r_rows, o_cols].rearrange("p r (q i) -> p q r i", i=4)
+                    dst = woven[:, o_cols, r_rows].rearrange("p (q i) r -> p q r i", i=4)
                     if engines[n % len(engines)] == "v":
-                        nc.vector.tensor_copy(out=woven[:, o_cols, r_rows], in_=src)
+                        nc.vector.tensor_copy(out=dst, in_=src)
                     else:
-                        nc.scalar.copy(out=woven[:, o_cols, r_rows], in_=src)
+                        nc.scalar.copy(out=dst, in_=src)
                 nc.sync.dma_start(out=out[b * P : (b + 1) * P, o_cols, :], in_=woven[:, o_cols, :])
 
         clip(0)

@@ -99,7 +99,7 @@ def tile_bsplinekanlayer_kernel(tc, x, coeff, base_weight, knots, grad_out, out)
 
         def regroup_g(c):
             nc.vector.tensor_copy(
-                out=g_grp[:, c].rearrange("p (q i) j -> p q j i", i=4), in_=g_raw[:, c].rearrange("p j (q i) -> p q j i", i=4)
+                out=g_grp[:, c].rearrange("p (q i) j -> p q j i", i=8), in_=g_raw[:, c].rearrange("p j (q i) -> p q j i", i=8)
             )
 
         def quantise_g(c):
@@ -122,8 +122,8 @@ def tile_bsplinekanlayer_kernel(tc, x, coeff, base_weight, knots, grad_out, out)
             h = u % PER_BLOCK
             t["xc"] = two.tile([P, W], BF16, name="xc")
             nc.vector.tensor_scalar(
-                out=t["xc"][:].rearrange("p (q i j) -> p q j i", i=4, j=PACK),
-                in0=x_raw[:, :, b, h * HALF : (h + 1) * HALF, :].rearrange("p j c (q i) -> p (c q) j i", i=4),
+                out=t["xc"][:].rearrange("p (q i j) -> p q j i", i=8, j=PACK),
+                in0=x_raw[:, :, b, h * HALF : (h + 1) * HALF, :].rearrange("p j c (q i) -> p (c q) j i", i=8),
                 scalar1=-1.0,
                 scalar2=1.0,
                 op0=ALU.max,

import math
from contextlib import ExitStack

import concourse.mybir as mybir
from concourse.masks import make_identity

F32 = mybir.dt.float32
BF16 = mybir.dt.bfloat16
U32 = mybir.dt.uint32
U8 = mybir.dt.uint8
E4M3X4 = mybir.dt.float8_e4m3fn_x4
E5M2X4 = mybir.dt.float8_e5m2_x4
ALU = mybir.AluOpType
ACT = mybir.ActivationFunctionType

P = 128
PACK = 4
TOKENS = 2048
NI = 512
NO = 512
NB = 8
PASSES = TOKENS // (P * PACK)
FLOPS = 2 * TOKENS * NI * NB * NO
BYTES = 2 * TOKENS * NI + 2 * TOKENS * NO + 4 * NI * NO * NB

KNOTS = (
    -2.203125,
    -1.796875,
    -1.3984375,
    -1.0,
    -0.6015625,
    -0.2001953125,
    0.2001953125,
    0.6015625,
    1.0,
    1.3984375,
    1.796875,
    2.203125,
)


def power_coefficient(r, j):
    tj = KNOTS[r + j]
    prod = 1.0
    for other in range(5):
        if other != j:
            prod = prod * (tj - KNOTS[r + other])
    return (KNOTS[r + 4] - KNOTS[r]) / prod


def tile_bsplinekanlayer_kernel(tc, x, coeff, base_weight, knots, grad_out, out):
    nc = tc.nc
    t6 = KNOTS[6]
    t7 = KNOTS[7]
    HALF = 2
    W = HALF * P * PACK
    BLOCKS = NI // P
    UNITS = BLOCKS * PASSES // HALF
    PER_BLOCK = PASSES // HALF

    def c2(r, j):
        return 2.0 * power_coefficient(r, j)

    with ExitStack() as ctx:
        ctx.enter_context(tc.manual_schedule())
        keep = ctx.enter_context(tc.tile_pool(name="keep", bufs=1))
        two = ctx.enter_context(tc.tile_pool(name="two", bufs=2))
        three = ctx.enter_context(tc.tile_pool(name="three", bufs=3))
        upool = ctx.enter_context(tc.tile_pool(name="upool", bufs=3))
        four_bufs = ctx.enter_context(tc.tile_pool(name="four_bufs", bufs=4))
        psum = ctx.enter_context(tc.psum_pool(name="psum", bufs=6))
        psum_sum = ctx.enter_context(tc.psum_pool(name="psum_sum", bufs=2))

        x_raw = keep.tile([P, PACK, NI // P, PASSES, P], BF16)
        g_codes = keep.tile([P, PASSES, NO], U32, align_bytes=64)
        g_scales = keep.tile([P, PASSES, NO], U8, align_bytes=64)
        g_raw = keep.tile([P, PASSES, PACK, NO], BF16, tag="planes", align_bytes=64)
        g_grp = keep.tile([P, PASSES, NO, PACK], BF16, tag="woven", align_bytes=64)
        def load_x(b):
            for c in range(PASSES):
                nc.sync.dma_start(
                    out=x_raw[:, :, b, c, :],
                    in_=x[c * P * PACK : (c + 1) * P * PACK, b * P : (b + 1) * P].rearrange("(p j) i -> p j i", j=PACK),
                )

        load_x(0)
        for c in range(PASSES):
            nc.sync.dma_start(
                out=g_raw[:, c],
                in_=grad_out[c * P * PACK : (c + 1) * P * PACK, :].rearrange("(p j) o -> p j o", j=PACK),
            )
        for b in range(1, NI // P):
            load_x(b)

        diag = [keep.tile([P, P], F32, name="diag%d" % n) for n in range(3)]
        make_identity(nc, diag[0][:])
        nc.scalar.mul(out=diag[1][:], in_=diag[0][:], mul=c2(5, 1) / c2(6, 0))
        nc.scalar.mul(out=diag[2][:], in_=diag[0][:], mul=c2(5, 2) / c2(6, 0))

        def regroup_g(c):
            nc.vector.tensor_copy(
                out=g_grp[:, c].rearrange("p (q i) j -> p q j i", i=8), in_=g_raw[:, c].rearrange("p j (q i) -> p q j i", i=8)
            )

        def quantise_g(c):
            nc.vector.quantize_mx(
                out=g_codes[:, c, :].bitcast(E5M2X4),
                scales=g_scales[:, c, :],
                in_=g_grp[:, c].rearrange("p o j -> p (o j)"),
            )

        tiles = [dict() for u in range(UNITS)]
        acc = {}
        CUBES = (("y7", -t7, 1.0), ("y6", -t6, 1.0), ("y5", t6, math.sqrt(c2(5, 0))), ("y8", -1.0, math.sqrt(c2(4, 4))))

        def axpy(dst, a, factor, b, op1):
            nc.vector.scalar_tensor_tensor(out=dst, in0=a, scalar=factor, in1=b, op0=ALU.mult, op1=op1)

        def clip(u):
            t = tiles[u]
            b = u // PER_BLOCK
            h = u % PER_BLOCK
            t["xc"] = two.tile([P, W], BF16, name="xc")
            nc.vector.tensor_scalar(
                out=t["xc"][:].rearrange("p (q i j) -> p q j i", i=8, j=PACK),
                in0=x_raw[:, :, b, h * HALF : (h + 1) * HALF, :].rearrange("p j c (q i) -> p (c q) j i", i=8),
                scalar1=-1.0,
                scalar2=1.0,
                op0=ALU.max,
                op1=ALU.min,
            )

        def sign(u):
            t = tiles[u]
            t["s"] = three.tile([P, W], BF16, name="s")
            nc.vector.tensor_scalar(
                out=t["s"][:], in0=t["xc"][:], scalar1=0.0, scalar2=0.5, op0=ALU.is_ge, op1=ALU.subtract
            )

        def absolute(u):
            t = tiles[u]
            t["z"] = two.tile([P, W], BF16, name="z")
            nc.scalar.activation(out=t["z"][:], in_=t["xc"][:], func=ACT.Abs)

        def squares(u):
            t = tiles[u]
            y76 = two.tile([P, 2, W], F32, name="y76")
            t["y76"] = y76
            t["y7"] = y76[:, 0, :]
            t["y6"] = y76[:, 1, :]
            y5 = two.tile([P, W], F32, name="y5")
            t["y5"] = y5[:]
            y8 = two.tile([P, W], F32, name="y8")
            t["y8"] = y8[:]
            for name, shift, scale in CUBES:
                nc.scalar.activation(out=t[name], in_=t["z"][:], func=ACT.Square, bias=scale * shift, scale=scale)

        def cubes(u, first, count):
            t = tiles[u]
            for name, shift, scale in CUBES[first : first + count]:
                nc.vector.scalar_tensor_tensor(
                    out=t[name], in0=t["z"][:], scalar=shift, in1=t[name], op0=ALU.add, op1=ALU.mult
                )

        def relus(u):
            t = tiles[u]
            t["f"] = two.tile([P, 6, W], BF16, name="f")
            rising = upool.tile([P, 2, W], F32, name="u")
            falling = upool.tile([P, 2, W], F32, name="u")
            t["u7"] = rising[:, 0, :]
            t["u6"] = rising[:, 1, :]
            t["w7"] = falling[:, 0, :]
            t["w6"] = falling[:, 1, :]
            nc.scalar.activation(out=rising[:], in_=t["y76"][:], func=ACT.Relu, scale=c2(6, 0))
            nc.scalar.activation(out=falling[:], in_=t["y76"][:], func=ACT.Relu, scale=-c2(3, 4))
            nc.scalar.activation(out=t["f"][:, 0, :], in_=t["y7"], func=ACT.Relu, scale=c2(7, 0))
            nc.scalar.mul(out=t["f"][:, 3, :], in_=t["w6"], mul=-c2(2, 4) / c2(3, 4))

        def add_function_5(u):
            t = tiles[u]
            t["sum5"] = []
            for n in range(W // NO):
                cols = slice(n * NO, (n + 1) * NO)
                bank = psum_sum.tile([P, NO], F32, name="sum5")
                for k, name in enumerate(("y5", "u6", "u7")):
                    nc.tensor.matmul(out=bank[:], lhsT=diag[k][:], rhs=t[name][:, cols], start=(k == 0), stop=(k == 2))
                t["sum5"].append(bank)

        def combine_a(u):
            t = tiles[u]
            t4 = two.tile([P, W], F32, name="t4")
            axpy(t4[:], t["w6"], c2(4, 2) / c2(3, 4), t["y8"], ALU.subtract)
            axpy(t["f"][:, 1, :], t["u7"], c2(6, 1) / c2(6, 0), t["u6"], ALU.add)
            axpy(t["f"][:, 2, :], t["w6"], -c2(3, 3) / c2(3, 4), t["w7"], ALU.subtract)
            axpy(t["f"][:, 4, :], t["w7"], c2(4, 3) / c2(3, 4), t4[:], ALU.add)

        def times_sign(u, all_on_vector):
            t = tiles[u]
            t["p"] = two.tile([P, 6, W], BF16, name="p")
            nc.vector.tensor_tensor(
                out=t["p"][:, 0:5, :], in0=t["f"][:, 0:5, :], in1=t["s"][:].unsqueeze(1).to_broadcast([P, 5, W]), op=ALU.mult
            )
            t["four_a"] = three.tile([P, 4, W], BF16, name="four", align_bytes=64)
            if all_on_vector:
                nc.vector.tensor_scalar(
                    out=t["four_a"][:, 0:2, :], in0=t["p"][:, 0:2, :], scalar1=0.0, scalar2=None, op0=ALU.max
                )
            if all_on_vector:
                nc.vector.tensor_scalar(
                    out=t["four_a"][:, 2:4, :],
                    in0=t["p"][:, 0:2, :],
                    scalar1=-1.0,
                    scalar2=0.0,
                    op0=ALU.mult,
                    op1=ALU.max,
                )

        def round_function_5(u):
            t = tiles[u]
            for n in range(W // NO):
                nc.scalar.copy(out=t["f"][:, 5, n * NO : (n + 1) * NO], in_=t["sum5"][n][:])

        def combine_b(u):
            t = tiles[u]
            nc.vector.tensor_tensor(out=t["p"][:, 5, :], in0=t["f"][:, 5, :], in1=t["s"][:], op=ALU.mult)

        def combine_b2(u):
            t = tiles[u]
            t["four_b"] = three.tile([P, 4, W], BF16, name="four", align_bytes=64)
            nc.vector.tensor_tensor(out=t["four_b"][:, 0:2, :], in0=t["p"][:, 4:6, :], in1=t["p"][:, 2:4, :], op=ALU.max)

        def combine_c(u):
            t = tiles[u]
            nc.vector.tensor_tensor(out=t["four_b"][:, 2:4, :], in0=t["p"][:, 4:6, :], in1=t["p"][:, 2:4, :], op=ALU.min)

        def scalar_has_room(step):
            return (step < 3 or step + 2 >= UNITS) and step != UNITS - 1

        def mirror_on_scalar(u):
            t = tiles[u]
            nc.scalar.activation(out=t["four_a"][:, 2:4, :], in_=t["p"][:, 0:2, :], func=ACT.Relu, scale=-1.0)
            nc.scalar.activation(out=t["four_a"][:, 0:2, :], in_=t["p"][:, 0:2, :], func=ACT.Relu)

        def mirror_on_vector(u):
            t = tiles[u]
            nc.vector.tensor_scalar(
                out=t["four_a"][:, 0:2, :], in0=t["p"][:, 0:2, :], scalar1=0.0, scalar2=None, op0=ALU.max
            )
            nc.vector.tensor_scalar(
                out=t["four_a"][:, 2:4, :],
                in0=t["p"][:, 0:2, :],
                scalar1=-1.0,
                scalar2=0.0,
                op0=ALU.mult,
                op1=ALU.max,
            )

        def multiply(u, which, rs, ks):
            t = tiles[u]
            h = u % PER_BLOCK
            for k in ks:
                if h == 0:
                    acc[rs[k]] = psum.tile([P, NO], F32, name="acc")
                for ci in range(HALF):
                    c = h * HALF + ci
                    cols = slice((k * HALF + ci) * P, (k * HALF + ci + 1) * P)
                    nc.tensor.matmul_mx(
                        out=acc[rs[k]][:],
                        lhsT=t["codes_" + which][:, cols].bitcast(E4M3X4),
                        lhsT_scale=t["scales_" + which][:, cols],
                        rhs=g_codes[:, c, :].bitcast(E5M2X4),
                        rhs_scale=g_scales[:, c, :],
                        start=(c == 0),
                        stop=(c == PASSES - 1),
                    )

        def quantise(u, which, first, count):
            t = tiles[u]
            key = "codes_" + which
            if key not in t:
                t[key] = four_bufs.tile([P, W], U32, name="codes", align_bytes=64)
                t["scales_" + which] = four_bufs.tile([P, W], U8, name="scales", align_bytes=64)
            words = slice(first * W // 4, (first + count) * W // 4)
            nc.vector.quantize_mx(
                out=t[key][:, words].bitcast(E4M3X4),
                scales=t["scales_" + which][:, words],
                in_=t[which][:, first : first + count, :].rearrange("p r n -> p (r n)"),
            )

        RS_A = (7, 6, 0, 1)
        RS_B = (4, 5, 3, 2)
        NEGATED = (3, 2)
        planes = {}

        def empty_banks(b, rs, engines):
            if b not in planes:
                planes[b] = keep.tile([P, NB, NO], F32, tag="planes", name="planes", align_bytes=64)
            for n, r in enumerate(rs):
                sign = -1.0 if r in NEGATED else 1.0
                if engines[n % len(engines)] == "v":
                    nc.vector.tensor_scalar(out=planes[b][:, r, :], in0=acc[r][:], scalar1=sign, scalar2=None, op0=ALU.mult)
                elif r in NEGATED:
                    nc.scalar.mul(out=planes[b][:, r, :], in_=acc[r][:], mul=sign)
                else:
                    nc.scalar.copy(out=planes[b][:, r, :], in_=acc[r][:])

        def weave_and_store(b, engines, stores):
            woven = keep.tile([P, NO, NB], F32, tag="woven", name="woven", align_bytes=64)
            piece = NO // stores
            for n in range(stores):
                o_cols = slice(n * piece, (n + 1) * piece)
                for rq in range(2):
                    r_rows = slice(rq * 4, (rq + 1) * 4)
                    src = planes[b][:, r_rows, o_cols].rearrange("p r (q i) -> p q r i", i=4)
                    dst = woven[:, o_cols, r_rows].rearrange("p (q i) r -> p q r i", i=4)
                    if engines[n % len(engines)] == "v":
                        nc.vector.tensor_copy(out=dst, in_=src)
                    else:
                        nc.scalar.copy(out=dst, in_=src)
                nc.sync.dma_start(out=out[b * P : (b + 1) * P, o_cols, :], in_=woven[:, o_cols, :])

        clip(0)
        clip(1)
        sign(0)
        sign(1)
        absolute(0)
        squares(0)
        absolute(1)
        squares(1)
        cubes(0, 0, 4)
        for c in range(PASSES):
            regroup_g(c)
        for c in range(PASSES):
            quantise_g(c)
        for t in range(UNITS):
            final = t == UNITS - 1
            closing = t >= 3 and t % PER_BLOCK == 1
            if t >= 1:
                combine_b(t - 1)
            if t + 2 < UNITS:
                clip(t + 2)
            if t >= 1:
                combine_b2(t - 1)
                combine_c(t - 1)
            relus(t)
            add_function_5(t)
            if t >= 1 and scalar_has_room(t):
                mirror_on_scalar(t - 1)
            if closing:
                empty_banks((t - 3) // PER_BLOCK, RS_A + RS_B[0:2], "s")
                multiply(t - 3, "four_b", RS_B, (2, 3))
                multiply(t - 2, "four_b", RS_B, (2, 3))
            if t + 2 < UNITS:
                absolute(t + 2)
                squares(t + 2)
            round_function_5(t)
            if closing:
                empty_banks((t - 3) // PER_BLOCK, RS_B[2:4], "s")
            if t >= 4 and t % PER_BLOCK == 0:
                weave_and_store((t - 4) // PER_BLOCK, "s", 2)
            if t + 1 < UNITS:
                cubes(t + 1, 0, 2)
            if t + 2 < UNITS:
                sign(t + 2)
            if t + 1 < UNITS:
                cubes(t + 1, 2, 1)
            combine_a(t)
            if t + 1 < UNITS:
                cubes(t + 1, 3, 1)
            times_sign(t, final)
            if t >= 1:
                quantise(t - 1, "four_a", 0, 4)
                multiply(t - 1, "four_a", RS_A, (0, 1, 2, 3))
                quantise(t - 1, "four_b", 0, 4)
                multiply(t - 1, "four_b", RS_B, (0, 1))
            if not final and not scalar_has_room(t + 1):
                mirror_on_vector(t)
            if final:
                quantise(t, "four_a", 0, 4)
                multiply(t, "four_a", RS_A, (0, 1, 2, 3))
                weave_and_store(BLOCKS - 2, "s", 2)
                empty_banks(BLOCKS - 1, RS_A, "s")
                multiply(t - 1, "four_b", RS_B, (2, 3))
                combine_b(t)
                combine_b2(t)
                quantise(t, "four_b", 0, 2)
                multiply(t, "four_b", RS_B, (0, 1))
                combine_c(t)
                quantise(t, "four_b", 2, 2)
                multiply(t, "four_b", RS_B, (2, 3))
                empty_banks(BLOCKS - 1, RS_B, "sv")
                weave_and_store(BLOCKS - 1, "vs", 4)
